import numpy as np
import ml_dtypes


def mxq(x, axis, fmt="e4m3"):
    dtype, down = {"e4m3": (ml_dtypes.float8_e4m3fn, 7), "e5m2": (ml_dtypes.float8_e5m2, 14)}[fmt]
    v = np.moveaxis(np.asarray(x, np.float32).astype(ml_dtypes.bfloat16).astype(np.float64), axis, -1)
    blocks = v.reshape(v.shape[:-1] + (-1, 32))
    amax = np.abs(blocks).max(-1, keepdims=True)
    byte = np.maximum(np.where(amax > 0, np.frexp(amax)[1] - 1 + 127, 0) - down, 1)
    scale = np.exp2(byte - 127.0)
    codes = (blocks / scale).astype(np.float32).astype(dtype).astype(np.float64)
    return np.moveaxis((codes * scale).reshape(v.shape), -1, axis)


WIDE = False


def mx_kscale(k):
    if not WIDE:
        return np.ones(k)
    levels = np.array([18, -18])
    if k % 512:
        return np.exp2(np.random.permutation(np.resize(levels, k // 32))).repeat(32)
    a = np.empty((k // 512, 16))
    for p in range(k // 512):
        a[p, :8] = np.random.permutation(np.resize(levels, 8))
        for g in range(8):
            far = levels[np.abs(levels - a[p, g]) >= 10]
            a[p, g + 8] = far[np.random.randint(len(far))]
    return np.exp2(a.ravel()).repeat(32)


BF16 = ml_dtypes.bfloat16


def bf(x):
    return np.asarray(x, np.float32).astype(BF16)


def f64(x):
    return np.asarray(x).astype(np.float64)


B, D_IN, H1, H2, LAT, NQ, NL, NA = 2048, 4096, 2048, 1024, 512, 512, 2, 3


def circuit(th, P):
    ar, ai = np.cos(0.5 * th), np.zeros_like(th)
    br, bi = np.sin(0.5 * th), np.zeros_like(th)
    for l in range(NL):
        rx, ry, rz = P[l].T
        c, s = np.cos(0.5 * rx), np.sin(0.5 * rx)
        ar, ai, br, bi = c * ar + s * bi, c * ai - s * br, s * ai + c * br, c * bi - s * ar
        c, s = np.cos(0.5 * ry), np.sin(0.5 * ry)
        ar, ai, br, bi = c * ar - s * br, c * ai - s * bi, s * ar + c * br, s * ai + c * bi
        c, s = np.cos(0.5 * rz), np.sin(0.5 * rz)
        ar, ai, br, bi = c * ar + s * ai, c * ai - s * ar, c * br - s * bi, c * bi + s * br
    return (ar * ar + ai * ai) - (br * br + bi * bi)


def rotate(x, y, z, P):
    for l in range(NL):
        rx, ry, rz = P[l].T
        c, s = np.cos(rx), np.sin(rx)
        y, z = c * y - s * z, s * y + c * z
        c, s = np.cos(ry), np.sin(ry)
        x, z = c * x + s * z, c * z - s * x
        c, s = np.cos(rz), np.sin(rz)
        x, y = c * x - s * y, s * x + c * y
    return z


def setup_inputs():
    s = mx_kscale(B)[:, None]
    u = mx_kscale(H2)
    v = mx_kscale(NQ)[:, None]
    h0 = bf(np.maximum(np.random.standard_normal((B, H2)), 0.0))
    we0 = bf(np.random.standard_normal((NQ, H2)) * 1.4 / np.sqrt(H2))
    be3 = bf(np.random.standard_normal(NQ) * 0.3)
    P = bf(np.random.standard_normal((NL, NQ, NA)))
    wd0 = bf(np.random.standard_normal((H2, NQ)) * 1.7 / np.sqrt(NQ))
    bd1 = bf(np.random.standard_normal(H2) * 0.3)
    g = bf(2.0 * np.random.standard_normal((B, H2)) * np.exp2(np.random.randint(-6, 1, (B, 1))) / s * u)
    th = f64(h0) @ f64(we0).T + f64(be3)
    y2 = circuit(th, f64(P)) @ f64(wd0).T + f64(bd1)
    return {"h_enc2": bf(f64(h0) * s), "We3": bf(f64(we0) / v), "be3": be3, "P": P,
            "Wd1": bf(f64(wd0) * v.T / u[:, None]), "bd1": bd1,
            "th": np.asarray(th, np.float32), "y2": np.asarray(y2, np.float32), "grad_out": g}


def reference(h_enc2, We3, be3, P, Wd1, bd1, th, y2, grad_out):
    dz2 = f64(grad_out) * (f64(y2) > 0.0)
    dh = mxq(dz2, 1, "e5m2") @ mxq(f64(Wd1), 0, "e4m3")
    pf = f64(P)
    zero, one = np.zeros(NQ), np.ones(NQ)
    ca = rotate(zero, zero, one, pf)
    sa = rotate(one, zero, zero, pf)
    tf = f64(th)
    dz1 = dh * (sa * np.cos(tf) - ca * np.sin(tf))
    dx = mxq(dz1, 1, "e5m2") @ mxq(f64(We3), 0, "e4m3")
    dw = mxq(dz1, 0, "e5m2").T @ mxq(f64(h_enc2), 0, "e4m3")
    return dx, dw

@@ -1,0 +1,543 @@
+import math
+from contextlib import ExitStack
+
+import concourse.mybir as mybir
+from concourse.masks import make_identity
+
+B, H2, NQ = 2048, 1024, 512
+FLOPS = 3 * 2 * B * H2 * NQ
+BYTES = 2 * (2 * B * H2 + 2 * H2 * NQ + 2 * NQ * 3) + 4 * (B * NQ + B * H2) + 4 * (B * H2 + NQ * H2)
+
+F32 = mybir.dt.float32
+BF16 = mybir.dt.bfloat16
+I32 = mybir.dt.int32
+U32 = mybir.dt.uint32
+U8 = mybir.dt.uint8
+E4 = mybir.dt.float8_e4m3fn_x4
+E5 = mybir.dt.float8_e5m2_x4
+ALU = mybir.AluOpType
+ACT = mybir.ActivationFunctionType
+
+P = 128
+GROUPS = 4
+TWO_PI = 2.0 * math.pi
+TILT_TAN = 0.75
+TILT = 0.6435011087932844
+TILT_COS = 0.8
+GUESS = 0.999 * math.pi
+
+
+def tile_unifiedautoencodernet_pa_v_kernel(tc, h_enc2, We3, be3, Pang, Wd1, bd1, th, y2, grad_out, out_0, out_1):
+    nc = tc.nc
+    vec, act, pe = nc.vector, nc.scalar, nc.tensor
+
+    y_v = y2.rearrange("(g p u e) h -> g u p e h", p=P, u=2, e=2)
+    g_v = grad_out.rearrange("(g p u e) h -> g u p e h", p=P, u=2, e=2)
+    o0_v = out_0.rearrange("(g p u e) h -> g u p e h", p=P, u=2, e=2)
+    th_v = th.rearrange("(g p j) q -> g p j q", p=P, j=4)
+    h_v = h_enc2.rearrange("(g p j) h -> g p j h", p=P, j=4)
+    wd_v = Wd1.rearrange("(c p j) q -> c p j q", p=P, j=4)
+    we_v = We3.rearrange("(g t i) h -> i g t h", t=4, i=8)
+
+    with ExitStack() as ctx:
+        sb = ctx.enter_context(tc.tile_pool(name="sb", bufs=1))
+        ps = ctx.enter_context(tc.psum_pool(name="ps", bufs=1))
+        ctx.enter_context(tc.manual_schedule())
+
+        def sbt(tag, shape, dtype, bufs=1):
+            return sb.tile(shape, dtype, name=tag, tag=tag, bufs=bufs, align_bytes=64)
+
+        free_banks = list(range(8))
+
+        def take_bank(dtype=F32):
+            n = free_banks[0]
+            free_banks.remove(n)
+            width = 512 if dtype == F32 else 1024
+            return n, ps.tile([P, width], dtype, name="bank%d" % n, tag="bank%d" % n, bufs=1)
+
+        def give_bank(n):
+            free_banks.append(n)
+
+        def copy(engine, out, in_):
+            if engine == "s":
+                act.copy(out=out, in_=in_)
+            else:
+                vec.tensor_copy(out=out, in_=in_)
+
+        def mx_tiles(tag, width, bufs):
+            return sbt(tag + "_codes", [P, width], U32, bufs), sbt(tag + "_scales", [P, width], U8, bufs)
+
+        def quantize(dst, cols, src, fmt):
+            vec.quantize_mx(out=dst[0][:, cols].bitcast(fmt), scales=dst[1][:, cols], in_=src)
+
+        def mm(bank, lhs, lcols, lfmt, rhs, rcols, rfmt, start, stop):
+            pe.matmul_mx(out=bank[:], lhsT=lhs[0][:, lcols].bitcast(lfmt), lhsT_scale=lhs[1][:, lcols],
+                         rhs=rhs[0][:, rcols].bitcast(rfmt), rhs_scale=rhs[1][:, rcols], start=start, stop=stop)
+
+        def cols(n, width):
+            return slice(n * width, (n + 1) * width)
+
+        warm = sbt("warm", [P, 1], F32)
+        vec.memset(warm[:], 0.0)
+        warm2 = sbt("warm2", [P, 1], F32)
+        act.activation(out=warm2[:], in_=warm[:], func=ACT.Sin)
+        ident = sbt("ident", [P, P], F32)
+        make_identity(nc, ident[:])
+        ident_bf = sbt("ident_bf", [P, P], BF16)
+        make_identity(nc, ident_bf[:])
+
+        y_t, g_t, th_t, h_t = {}, {}, {}, {}
+
+        def load_yg(g, u):
+            y_t[g, u] = sbt("y", [P, 2, H2], F32, 3)
+            nc.sync.dma_start(out=y_t[g, u][:], in_=y_v[g, u])
+            g_t[g, u] = sbt("g", [P, 2, H2], BF16, 4)
+            nc.sync.dma_start(out=g_t[g, u][:], in_=g_v[g, u])
+
+        def load_th(g):
+            th_t[g] = sbt("th", [P, 4, NQ], F32, 2)
+            nc.sync.dma_start(out=th_t[g][:], in_=th_v[g])
+
+        def load_h(g):
+            h_t[g] = sbt("h", [P, 4, H2], BF16, 2)
+            nc.sync.dma_start(out=h_t[g][:], in_=h_v[g])
+
+        ang = sbt("ang", [P, 2, 12], BF16)
+        nc.sync.dma_start(out=ang[:], in_=Pang.rearrange("l (p s) a -> p l (s a)", s=4))
+        wd_raw = sbt("stage", [P, 2, 4, NQ], BF16, 5)
+        we_raw = sbt("stage", [P, 4, H2], BF16, 5)
+
+        def load_we(i):
+            nc.sync.dma_start(out=we_raw[i:P:8, :, :], in_=we_v[i])
+
+        nc.sync.dma_start(out=wd_raw[:, 0], in_=wd_v[0])
+        load_th(0)
+        for i in range(8):
+            load_we(i)
+        load_yg(0, 0)
+        nc.sync.dma_start(out=wd_raw[:, 1], in_=wd_v[1])
+        load_yg(0, 1)
+        load_th(1)
+        load_yg(1, 0)
+        load_h(0)
+
+        small_n = [0]
+
+        def small(shape, dtype=F32):
+            small_n.append(0)
+            return sbt("small%d" % len(small_n), [P] + shape, dtype)
+
+        steps = []
+
+        def tt(a, b, op, shape, out=None):
+            res = small(shape)[:] if out is None else out
+            steps.append(lambda: vec.tensor_tensor(out=res, in0=a, in1=b, op=op))
+            return res
+
+        def ts(a, s1, s2, op0, op1, shape, dtype=F32, out=None):
+            res = small(shape, dtype)[:] if out is None else out
+            steps.append(lambda: vec.tensor_scalar(out=res, in0=a, scalar1=s1, scalar2=s2, op0=op0, op1=op1))
+            return res
+
+        def stt(a, s, b, op0, op1, shape, out=None):
+            res = small(shape)[:] if out is None else out
+            steps.append(lambda: vec.scalar_tensor_tensor(out=res, in0=a, scalar=s, in1=b, op0=op0, op1=op1))
+            return res
+
+        def scal(out, a, func, scale, bias):
+            steps.append(lambda: act.activation(out=out, in_=a, func=func, scale=scale, bias=bias))
+
+        def recip(a):
+            res = small([4])[:]
+            steps.append(lambda: vec.reciprocal(out=res, in_=a))
+            return res
+
+        def both(a):
+            return a.unsqueeze(1).to_broadcast([P, 2, 4])
+
+        pick_rows = sbt("pick_rows", [P, 512], BF16)
+        vec.tensor_copy(out=pick_rows[:].rearrange("p (t g a s) -> p t g a s", t=4, a=2, s=4),
+                        in_=ident_bf[:].rearrange("p (g t a) -> p t g a", t=4, a=2).unsqueeze(4).to_broadcast([P, 4, 16, 2, 4]))
+        pick_slot = small([4])
+        vec.tensor_reduce(out=pick_slot[:], in_=ident_bf[:].rearrange("p (m s) -> p s m", s=4), axis=mybir.AxisListType.X, op=ALU.add)
+        n, bank = take_bank()
+        for t in range(4):
+            pe.matmul(bank[:, cols(t, 24)], lhsT=pick_rows[:, cols(t, P)], rhs=ang[:].rearrange("p l x -> p (l x)"), start=True, stop=True)
+        picked = small([8, 4, 3])
+        vec.tensor_tensor(out=picked[:], in0=bank[:, 0:96].rearrange("p (x s a) -> p x s a", s=4, a=3),
+                          in1=pick_slot[:].unsqueeze(1).unsqueeze(3).to_broadcast([P, 8, 4, 3]), op=ALU.mult)
+        give_bank(n)
+        ang_own = small([8, 3])
+        vec.tensor_reduce(out=ang_own[:], in_=picked[:].rearrange("p x s a -> p x a s"), axis=mybir.AxisListType.X, op=ALU.add)
+        ang_flat = ang_own[:].rearrange("p x a -> p (x a)")
+        turns = small([2, 24], I32)
+        ts(ang_flat, 1.0 / TWO_PI, -0.25, ALU.mult, ALU.add, None, out=turns[:, 0, :])
+        ts(ang_flat, 1.0 / TWO_PI, 0.0, ALU.mult, ALU.add, None, out=turns[:, 1, :])
+        red = stt(turns[:], -TWO_PI, ang_flat.unsqueeze(1).to_broadcast([P, 2, 24]), ALU.mult, ALU.add, [2, 24])
+        trig = small([2, 24])
+        folded = small([2, 24])
+        scal(folded[:, 0, :], red[:, 0, :], ACT.Abs, 1.0, -0.5 * math.pi)
+        scal(folded[:, 1, :], red[:, 1, :], ACT.Abs, 1.0, 0.0)
+        scal(trig[:], folded[:], ACT.Sin, -1.0, 0.5 * math.pi)
+        sc = trig[:].rearrange("p w (s l a) -> p l a w s", l=2, a=3)
+        w1 = tt(both(sc[:, 1, 1, 1]), sc[:, 1, 0], ALU.mult, [2, 4])
+        pa = tt(both(sc[:, 1, 1, 0]), sc[:, 0, 2], ALU.mult, [2, 4])
+        pb = tt(both(w1[:, 0]), sc[:, 0, 2], ALU.mult, [2, 4])
+        pc = tt(both(w1[:, 1]), sc[:, 0, 1], ALU.mult, [2, 4])
+        wx2 = tt(pb[:, 0], pa[:, 1], ALU.subtract, [4])
+        wy2 = tt(pb[:, 1], pa[:, 0], ALU.add, [4])
+        pd = tt(both(wx2), sc[:, 0, 1], ALU.mult, [2, 4])
+        pe_ = tt(wy2, sc[:, 0, 0, 0], ALU.mult, [4])
+        yx = small([2, 4])
+        wz3 = tt(pd[:, 0], pc[:, 1], ALU.add, [4])
+        sa = stt(pd[:, 1], 1e-30, pc[:, 0], ALU.add, ALU.subtract, [4])
+        pf = tt(wz3, sc[:, 0, 0, 1], ALU.mult, [4])
+        ca = tt(pf, pe_, ALU.subtract, [4])
+        stt(sa, TILT_TAN, ca, ALU.mult, ALU.add, None, out=yx[:, 0, :])
+        stt(ca, -TILT_TAN, sa, ALU.mult, ALU.add, None, out=yx[:, 1, :])
+        mag = stt(yx[:], -1.0, yx[:], ALU.mult, ALU.max, [2, 4])
+        side = ts(yx[:, 1, :], 0.0, GUESS, ALU.is_ge, ALU.mult, [4])
+        den = tt(mag[:, 0], mag[:, 1], ALU.add, [4])
+        num = stt(side, -0.5 * GUESS, yx[:, 0, :], ALU.add, ALU.mult, [4])
+        rden = recip(den)
+        guess = tt(num, rden, ALU.mult, [4])
+        sc0 = small([2, 4])
+        scal(sc0[:, 0, :], guess, ACT.Sin, 1.0, 0.0)
+        scal(sc0[:, 1, :], guess, ACT.Sin, 1.0, 0.5 * math.pi)
+        gy = tt(both(yx[:, 0, :]), sc0[:], ALU.mult, [2, 4])
+        gx = tt(both(yx[:, 1, :]), sc0[:], ALU.mult, [2, 4])
+        dn = tt(gy[:, 0], gx[:, 1], ALU.add, [4])
+        nn = tt(gy[:, 1], gx[:, 0], ALU.subtract, [4])
+        rdn = recip(dn)
+        tan = tt(nn, rdn, ALU.mult, [4])
+        sq = tt(tan, tan, ALU.mult, [4])
+        h1 = ts(sq, -1.0 / 7.0, 1.0 / 5.0, ALU.mult, ALU.add, [4])
+        g1 = ts(sq, TILT_COS / 16.0, -TILT_COS / 8.0, ALU.mult, ALU.add, [4])
+        h2 = tt(h1, sq, ALU.mult, [4])
+        g2 = tt(g1, sq, ALU.mult, [4])
+        h3 = stt(h2, -1.0 / 3.0, sq, ALU.add, ALU.mult, [4])
+        g3 = stt(g2, 0.5 * TILT_COS, sq, ALU.add, ALU.mult, [4])
+        err = stt(h3, 1.0, tan, ALU.add, ALU.mult, [4])
+        pr = small([2, 4])
+        stt(g3, TILT_COS, dn, ALU.add, ALU.mult, None, out=pr[:, 1, :])
+        stt(guess, -TILT, err, ALU.add, ALU.add, None, out=pr[:, 0, :])
+
+        def run_steps(n):
+            for step in steps[:n]:
+                step()
+            for step in steps[:n]:
+                steps.remove(step)
+
+        wd_mx = [mx_tiles("wd%d" % c, 512, 1) for c in range(2)]
+        we_mx = mx_tiles("we", 1024, 1)
+        wd_grp, we_grp = {}, {}
+
+        def wd_interleave(c, engine):
+            wd_grp[c] = sbt("ag", [P, 2048], BF16)
+            copy(engine, wd_grp[c][:].rearrange("p (t g i j) -> p t g i j", t=4, i=8, j=4),
+                 wd_raw[:, c].rearrange("p j (g t i) -> p t g i j", t=4, i=8))
+
+        def wd_quantize(c):
+            quantize(wd_mx[c], cols(0, 512), wd_grp[c][:], E4)
+
+        def pe_interleave(dst, parts):
+            b, bank = take_bank(BF16)
+            for z in range(2):
+                pe.matmul(bank[:, cols(z, 512)].rearrange(parts[z][1], j=4, **parts[z][2]), lhsT=ident_bf[:], rhs=parts[z][0], start=True, stop=True)
+            act.copy(out=dst, in_=bank[:])
+            give_bank(b)
+
+        def wd_interleave_pe(c):
+            wd_grp[c] = sbt("bg", [P, 2048], BF16)
+            src = wd_raw[:, c].rearrange("p j (g t i) -> p t g i j", t=4, i=8)
+            for x in range(2):
+                pe_interleave(wd_grp[c][:, cols(x, 1024)], [(src[:, 2 * x + z], "p (g i j) -> p g i j", dict(i=8)) for z in range(2)])
+
+        def we_interleave(n):
+            we_grp[n] = sbt("hg", [P, 2048], BF16, 2)
+            act.copy(out=we_grp[n][:].rearrange("p (c t) -> p c t", t=4), in_=we_raw[:, :, cols(n, 512)].rearrange("p t c -> p c t"))
+
+        def we_quantize(n):
+            quantize(we_mx, cols(n, 512), we_grp[n][:], E4)
+
+        dz2_t, dzg, dz2_mx = {}, {}, {}
+
+        def mask(g, u):
+            dz2_t[g, u] = sbt("dz2", [P, 2 * H2], BF16, 2)
+            vec.scalar_tensor_tensor(out=dz2_t[g, u][:], in0=y_t[g, u][:].rearrange("p e h -> p (e h)"), scalar=0.0,
+                                     in1=g_t[g, u][:].rearrange("p e h -> p (e h)"), op0=ALU.is_gt, op1=ALU.mult)
+
+        def turn_dz2(g, u):
+            words = dz2_t[g, u][:].bitcast(F32)
+            for c in range(2):
+                if u == 0:
+                    dzg[g, c] = sbt("dzg", [P, 2048], BF16, 2)
+                n, bank = take_bank()
+                for e in range(2):
+                    for f in range(2):
+                        first = 512 * e + 256 * c + f
+                        pe.transpose(bank[:, cols(2 * e + f, P)], words[:, first:512 * e + 256 * (c + 1):2], ident[:])
+                act.copy(out=dzg[g, c][:].bitcast(F32)[:, cols(u, 512)].rearrange("p (m e f) -> p m e f", e=2, f=2),
+                         in_=bank[:].rearrange("p (e f m) -> p m e f", e=2, f=2))
+                give_bank(n)
+
+        def quant_dz2(g, c):
+            dz2_mx[g, c] = mx_tiles("dz2", 512, 2)
+            quantize(dz2_mx[g, c], cols(0, 512), dzg[g, c][:], E5)
+
+        k_t, r_t, ab_t, s_t, dh_t, dz1_t = {}, {}, {}, {}, {}, {}
+
+        def count_turns(g, js=slice(0, 4)):
+            if js.start == 0:
+                k_t[g] = sbt("k", [P, 4, NQ], I32)
+            vec.tensor_scalar(out=k_t[g][:, js], in0=th_t[g][:, js], scalar1=1.0 / TWO_PI, scalar2=-TILT / TWO_PI, op0=ALU.mult, op1=ALU.add)
+
+        def reduce_angle(g, t, xs=slice(0, 64)):
+            if xs.start == 0:
+                r_t[g, t] = sbt("r", [P, NQ], F32, 4)
+            pick = "p j (g t i) -> p t (j g) i"
+            vec.scalar_tensor_tensor(out=r_t[g, t][:].rearrange("p (x i) -> p x i", i=8)[:, xs],
+                                     in0=k_t[g][:].rearrange(pick, t=4, i=8)[:, t, xs], scalar=-TWO_PI,
+                                     in1=th_t[g][:].rearrange(pick, t=4, i=8)[:, t, xs], op0=ALU.mult, op1=ALU.add)
+
+        def sine(g, t):
+            n, bank = take_bank()
+            for j in range(4):
+                pe.transpose(bank[:, cols(j, P)], r_t[g, t][:, cols(j, P)], ident[:])
+            tp, x = divmod(t, 2)
+            if x == 0:
+                ab_t[g, tp] = sbt("ab", [P, 1024], F32)
+            act.activation(out=ab_t[g, tp][:, cols(x, 512)].rearrange("p (u m e) -> p u m e", u=2, e=2),
+                           in_=bank[:].rearrange("p (u e m) -> p u m e", u=2, e=2), func=ACT.Abs, bias=pr[:, 0, t:t + 1])
+            give_bank(n)
+            if x == 1:
+                s_t[g, tp] = sbt("s", [P, 1024], F32, 2)
+                act.activation(out=s_t[g, tp][:], in_=ab_t[g, tp][:], func=ACT.Sin, scale=-1.0, bias=0.5 * math.pi)
+
+        def dh_mm(g, t):
+            dh_t[g, t] = take_bank()
+            for c in range(2):
+                mm(dh_t[g, t][1], wd_mx[c], cols(t, P), E4, dz2_mx[g, c], cols(0, 512), E5, c == 0, c == 1)
+
+        def make_dz1(g, t):
+            if t == 0:
+                dz1_t[g] = sbt("dz1", [P, 2048], BF16)
+            n, bank = dh_t[g, t]
+            vec.scalar_tensor_tensor(out=dz1_t[g][:, cols(t, 512)], in0=bank[:], scalar=pr[:, 1, t:t + 1],
+                                     in1=s_t[g, t // 2][:, cols(t % 2, 512)], op0=ALU.mult, op1=ALU.mult)
+            give_bank(n)
+
+        hg, h_mx, ag, bg, a_mx, b_mx = {}, {}, {}, {}, {}, {}
+
+        def h_interleave(g, n):
+            src = h_t[g][:].rearrange("p j c -> p c j")
+            hg[g, n] = sbt("hg", [P, 2048], BF16, 2)
+            for x in range(2):
+                pe_interleave(hg[g, n][:, cols(x, 1024)], [(src[:, cols(4 * n + 2 * x + z, P), :], "p (c j) -> p c j", {}) for z in range(2)])
+
+        def h_quantize(g, n):
+            if n == 0:
+                h_mx[g] = mx_tiles("h", 1024, 4)
+            quantize(h_mx[g], cols(n, 512), hg[g, n][:], E4)
+
+        def a_interleave(g, us):
+            if us.start == 0:
+                ag[g] = sbt("ag", [P, 2048], BF16)
+            dst = ag[g][:].rearrange("p (u e m t) -> p u e m t", u=2, e=2, t=4)
+            src = dz1_t[g][:].rearrange("p (t u m e) -> p u e m t", t=4, u=2, e=2)
+            vec.tensor_copy(out=dst[:, us], in_=src[:, us])
+
+        def b_turn(g, tp, engine):
+            if tp == 0:
+                bg[g] = sbt("bg", [P, 2048], BF16)
+            words = dz1_t[g][:].bitcast(F32)
+            n, bank = take_bank()
+            for x in range(4):
+                pe.transpose(bank[:, cols(x, P)], words[:, cols(4 * tp + x, P)], ident[:])
+            dst = bg[g][:].bitcast(F32).rearrange("p (g t i u) -> p g t i u", t=4, i=8, u=2)
+            copy(engine, dst[:, :, 2 * tp:2 * tp + 2], bank[:].rearrange("p (t u g i) -> p g t i u", t=2, u=2, i=8))
+            give_bank(n)
+
+        def a_quantize(g, us):
+            if us.start == 0:
+                a_mx[g] = mx_tiles("a", 512, 1)
+            quantize(a_mx[g], slice(256 * us.start, 256 * us.stop), ag[g][:, 1024 * us.start:1024 * us.stop], E5)
+
+        def b_quantize(g):
+            b_mx[g] = mx_tiles("b", 512, 4)
+            quantize(b_mx[g], cols(0, 512), bg[g][:], E5)
+
+        o_t = {}
+
+        def out0_tile(g, x, engine):
+            j, n = divmod(x, 2)
+            u, e = divmod(j, 2)
+            if e == 0 and n == 0:
+                o_t[g, u] = sbt("stage", [P, 2, H2], F32, 5)
+            b, bank = take_bank()
+            mm(bank, a_mx[g], cols(j, P), E5, we_mx, cols(n, 512), E4, True, True)
+            copy(engine, o_t[g, u][:, e, cols(n, 512)], bank[:])
+            give_bank(b)
+            if g == GROUPS - 1 and n == 1:
+                nc.sync.dma_start(out=o0_v[g, u][:, e], in_=o_t[g, u][:, e])
+            elif e == 1 and n == 1:
+                nc.sync.dma_start(out=o0_v[g, u], in_=o_t[g, u][:])
+
+        o1_banks = {}
+
+        def out1_open(qt):
+            for n in range(2):
+                o1_banks[qt, n] = take_bank()
+                for g in range(GROUPS - 1):
+                    mm(o1_banks[qt, n][1], b_mx[g], cols(qt, P), E5, h_mx[g], cols(n, 512), E4, g == 0, False)
+
+        def out1_close(qt):
+            g = GROUPS - 1
+            res = sbt("stage", [P, H2], F32, 5)
+            for n in range(2):
+                b, bank = o1_banks[qt, n]
+                mm(bank, b_mx[g], cols(qt, P), E5, h_mx[g], cols(n, 512), E4, False, True)
+                copy("sv"[n], res[:, cols(n, 512)], bank[:])
+                give_bank(b)
+            nc.sync.dma_start(out=out_1[cols(qt, P), :], in_=res[:])
+
+        both_halves = slice(0, 2)
+        run_steps(6)
+        wd_interleave(0, "s")
+        run_steps(9)
+        for j in range(4):
+            count_turns(0, slice(j, j + 1))
+            run_steps(2)
+        wd_quantize(0)
+        run_steps(5)
+        we_interleave(0)
+        we_interleave(1)
+        for t in range(4):
+            for x in range(2):
+                reduce_angle(0, t, slice(32 * x, 32 * x + 32))
+                run_steps(2)
+        run_steps(len(steps))
+        mask(0, 0)
+        load_yg(1, 1)
+        load_h(1)
+        wd_interleave_pe(1)
+        turn_dz2(0, 0)
+        sine(0, 0)
+        sine(0, 1)
+        we_quantize(0)
+        mask(0, 1)
+        load_yg(2, 0)
+        turn_dz2(0, 1)
+        sine(0, 2)
+        sine(0, 3)
+        we_quantize(1)
+        wd_quantize(1)
+        count_turns(1)
+        quant_dz2(0, 0)
+        quant_dz2(0, 1)
+        for t in range(4):
+            dh_mm(0, t)
+        mask(1, 0)
+        h_interleave(0, 0)
+        h_interleave(0, 1)
+        load_h(2)
+        load_th(2)
+        load_yg(2, 1)
+        for t in range(4):
+            make_dz1(0, t)
+        turn_dz2(1, 0)
+
+        for i in range(1, GROUPS):
+            last = i == GROUPS - 1
+            for t in range(4):
+                reduce_angle(i, t)
+            if i == 1:
+                sine(i, 0)
+                sine(i, 1)
+                h_quantize(0, 0)
+                h_quantize(0, 1)
+                mask(1, 1)
+                load_yg(3, 0)
+                b_turn(i - 1, 0, "s")
+                b_turn(i - 1, 1, "s")
+                h_interleave(1, 0)
+                turn_dz2(i, 1)
+                h_interleave(1, 1)
+                load_h(3)
+                load_th(3)
+                a_interleave(i - 1, both_halves)
+                b_quantize(i - 1)
+            else:
+                turn_dz2(i, 1)
+                sine(i, 0)
+                sine(i, 1)
+                a_interleave(i - 1, both_halves)
+                b_turn(i - 1, 0, "s")
+                b_turn(i - 1, 1, "s")
+            sine(i, 2)
+            sine(i, 3)
+            quant_dz2(i, 0)
+            quant_dz2(i, 1)
+            a_quantize(i - 1, both_halves)
+            dh_mm(i, 0)
+            dh_mm(i, 1)
+            if last:
+                break
+            for x in range(4):
+                out0_tile(i - 1, x, "s")
+            if i > 1:
+                b_quantize(i - 1)
+            h_quantize(i, 0)
+            h_quantize(i, 1)
+            h_interleave(i + 1, 0)
+            mask(i + 1, 0)
+            if i == 1:
+                load_yg(3, 1)
+            make_dz1(i, 0)
+            make_dz1(i, 1)
+            turn_dz2(i + 1, 0)
+            dh_mm(i, 2)
+            dh_mm(i, 3)
+            count_turns(i + 1)
+            for x in range(4, 8):
+                out0_tile(i - 1, x, "s")
+            h_interleave(i + 1, 1)
+            mask(i + 1, 1)
+            make_dz1(i, 2)
+            make_dz1(i, 3)
+
+        g = GROUPS - 1
+        b_quantize(g - 1)
+        for x in range(4):
+            out0_tile(g - 1, x, "v")
+        out0_tile(g - 1, 4, "s")
+        out0_tile(g - 1, 5, "s")
+        out1_open(0)
+        out0_tile(g - 1, 6, "s")
+        out0_tile(g - 1, 7, "s")
+        h_quantize(g, 0)
+        h_quantize(g, 1)
+        dh_mm(g, 2)
+        dh_mm(g, 3)
+        make_dz1(g, 0)
+        make_dz1(g, 1)
+        b_turn(g, 0, "s")
+        make_dz1(g, 2)
+        make_dz1(g, 3)
+        b_turn(g, 1, "s")
+        out1_open(1)
+        a_interleave(g, slice(0, 1))
+        a_quantize(g, slice(0, 1))
+        a_interleave(g, slice(1, 2))
+        b_quantize(g)
+        for x in range(4):
+            out0_tile(g, x, "s")
+        a_quantize(g, slice(1, 2))
+        out1_close(0)
+        out1_close(1)
+        for x in range(4, 8):
+            out0_tile(g, x, "sv"[x % 2])
+        out1_open(2)
+        out1_close(2)
+        out1_open(3)
+        out1_close(3)

@@ -233,29 +233,19 @@ def tile_unifiedautoencodernet_pa_v_kernel(tc, h_enc2, We3, be3, Pang, Wd1, bd1,
         wd_grp, we_grp = {}, {}
 
         def wd_interleave(c, engine):
-            wd_grp[c] = sbt("ag", [P, 2048], BF16)
+            wd_grp[c] = sbt("ag" if c == 0 else "bg", [P, 2048], BF16)
             copy(engine, wd_grp[c][:].rearrange("p (t g i j) -> p t g i j", t=4, i=8, j=4),
                  wd_raw[:, c].rearrange("p j (g t i) -> p t g i j", t=4, i=8))
 
         def wd_quantize(c):
             quantize(wd_mx[c], cols(0, 512), wd_grp[c][:], E4)
 
-        def pe_interleave(dst, parts):
-            b, bank = take_bank(BF16)
-            for z in range(2):
-                pe.matmul(bank[:, cols(z, 512)].rearrange(parts[z][1], j=4, **parts[z][2]), lhsT=ident_bf[:], rhs=parts[z][0], start=True, stop=True)
-            act.copy(out=dst, in_=bank[:])
-            give_bank(b)
-
-        def wd_interleave_pe(c):
-            wd_grp[c] = sbt("bg", [P, 2048], BF16)
-            src = wd_raw[:, c].rearrange("p j (g t i) -> p t g i j", t=4, i=8)
-            for x in range(2):
-                pe_interleave(wd_grp[c][:, cols(x, 1024)], [(src[:, 2 * x + z], "p (g i j) -> p g i j", dict(i=8)) for z in range(2)])
+        def interleave(engine, dst, src):
+            copy(engine, dst.rearrange("p (c i t) -> p c t i", i=4, t=4), src.rearrange("p t (c i) -> p c t i", i=4))
 
         def we_interleave(n):
             we_grp[n] = sbt("hg", [P, 2048], BF16, 2)
-            act.copy(out=we_grp[n][:].rearrange("p (c t) -> p c t", t=4), in_=we_raw[:, :, cols(n, 512)].rearrange("p t c -> p c t"))
+            interleave("s", we_grp[n][:], we_raw[:, :, cols(n, 512)])
 
         def we_quantize(n):
             quantize(we_mx, cols(n, 512), we_grp[n][:], E4)
@@ -329,11 +319,11 @@ def tile_unifiedautoencodernet_pa_v_kernel(tc, h_enc2, We3, be3, Pang, Wd1, bd1,
 
         hg, h_mx, ag, bg, a_mx, b_mx = {}, {}, {}, {}, {}, {}
 
-        def h_interleave(g, n):
-            src = h_t[g][:].rearrange("p j c -> p c j")
-            hg[g, n] = sbt("hg", [P, 2048], BF16, 2)
-            for x in range(2):
-                pe_interleave(hg[g, n][:, cols(x, 1024)], [(src[:, cols(4 * n + 2 * x + z, P), :], "p (c j) -> p c j", {}) for z in range(2)])
+        def h_interleave(g, x, engine):
+            n, z = divmod(x, 2)
+            if z == 0:
+                hg[g, n] = sbt("hg", [P, 2048], BF16, 2)
+            interleave(engine, hg[g, n][:, cols(z, 1024)], h_t[g][:, :, cols(x, 256)])
 
         def h_quantize(g, n):
             if n == 0:
@@ -420,7 +410,7 @@ def tile_unifiedautoencodernet_pa_v_kernel(tc, h_enc2, We3, be3, Pang, Wd1, bd1,
         mask(0, 0)
         load_yg(1, 1)
         load_h(1)
-        wd_interleave_pe(1)
+        wd_interleave(1, "s")
         turn_dz2(0, 0)
         sine(0, 0)
         sine(0, 1)
@@ -438,8 +428,9 @@ def tile_unifiedautoencodernet_pa_v_kernel(tc, h_enc2, We3, be3, Pang, Wd1, bd1,
         for t in range(4):
             dh_mm(0, t)
         mask(1, 0)
-        h_interleave(0, 0)
-        h_interleave(0, 1)
+        for x in range(3):
+            h_interleave(0, x, "s")
+        h_interleave(0, 3, "v")
         load_h(2)
         load_th(2)
         load_yg(2, 1)
@@ -460,9 +451,11 @@ def tile_unifiedautoencodernet_pa_v_kernel(tc, h_enc2, We3, be3, Pang, Wd1, bd1,
                 load_yg(3, 0)
                 b_turn(i - 1, 0, "s")
                 b_turn(i - 1, 1, "s")
-                h_interleave(1, 0)
+                h_interleave(1, 0, "s")
                 turn_dz2(i, 1)
-                h_interleave(1, 1)
+                h_interleave(1, 1, "s")
+                h_interleave(1, 2, "v")
+                h_interleave(1, 3, "v")
                 load_h(3)
                 load_th(3)
                 a_interleave(i - 1, both_halves)
@@ -485,11 +478,12 @@ def tile_unifiedautoencodernet_pa_v_kernel(tc, h_enc2, We3, be3, Pang, Wd1, bd1,
                 break
             for x in range(4):
                 out0_tile(i - 1, x, "s")
-            if i > 1:
-                b_quantize(i - 1)
             h_quantize(i, 0)
             h_quantize(i, 1)
-            h_interleave(i + 1, 0)
+            if i > 1:
+                b_quantize(i - 1)
+            h_interleave(i + 1, 0, "s")
+            h_interleave(i + 1, 1, "s")
             mask(i + 1, 0)
             if i == 1:
                 load_yg(3, 1)
@@ -501,12 +495,15 @@ def tile_unifiedautoencodernet_pa_v_kernel(tc, h_enc2, We3, be3, Pang, Wd1, bd1,
             count_turns(i + 1)
             for x in range(4, 8):
                 out0_tile(i - 1, x, "s")
-            h_interleave(i + 1, 1)
+            h_interleave(i + 1, 2, "v" if i == 2 else "s")
+            h_interleave(i + 1, 3, "v")
             mask(i + 1, 1)
             make_dz1(i, 2)
             make_dz1(i, 3)
 
         g = GROUPS - 1
+        h_quantize(g, 0)
+        h_quantize(g, 1)
         b_quantize(g - 1)
         for x in range(4):
             out0_tile(g - 1, x, "v")
@@ -515,8 +512,6 @@ def tile_unifiedautoencodernet_pa_v_kernel(tc, h_enc2, We3, be3, Pang, Wd1, bd1,
         out1_open(0)
         out0_tile(g - 1, 6, "s")
         out0_tile(g - 1, 7, "s")
-        h_quantize(g, 0)
-        h_quantize(g, 1)
         dh_mm(g, 2)
         dh_mm(g, 3)
         make_dz1(g, 0)

@@ -19,520 +19,509 @@ ALU = mybir.AluOpType
 ACT = mybir.ActivationFunctionType
 
 P = 128
-GROUPS = 4
+PASS = 512
+GROUPS = B // PASS
+LAST = GROUPS - 1
 TWO_PI = 2.0 * math.pi
-TILT_TAN = 0.75
+
 TILT = 0.6435011087932844
+TILT_TAN = 0.75
 TILT_COS = 0.8
-GUESS = 0.999 * math.pi
+GUESS_SPAN = 0.999 * math.pi
+TINY = 1e-30
+
+LEAD = 9
+WEAVE = 2
 
 
-def tile_unifiedautoencodernet_pa_v_kernel(tc, h_enc2, We3, be3, Pang, Wd1, bd1, th, y2, grad_out, out_0, out_1):
+def tile_unifiedautoencodernet_pa_v_kernel(tc, h_enc2, We3, be3, gate_angles, Wd1, bd1, th, y2, grad_out, out_0, out_1):
     nc = tc.nc
     vec, act, pe = nc.vector, nc.scalar, nc.tensor
+    on_vector, on_scalar = vec.tensor_copy, act.copy
 
-    y_v = y2.rearrange("(g p u e) h -> g u p e h", p=P, u=2, e=2)
-    g_v = grad_out.rearrange("(g p u e) h -> g u p e h", p=P, u=2, e=2)
-    o0_v = out_0.rearrange("(g p u e) h -> g u p e h", p=P, u=2, e=2)
-    th_v = th.rearrange("(g p j) q -> g p j q", p=P, j=4)
-    h_v = h_enc2.rearrange("(g p j) h -> g p j h", p=P, j=4)
-    wd_v = Wd1.rearrange("(c p j) q -> c p j q", p=P, j=4)
-    we_v = We3.rearrange("(g t i) h -> i g t h", t=4, i=8)
+    y2_hbm = y2.rearrange("(g p u e) h -> g u p e h", p=P, u=2, e=2)
+    grad_hbm = grad_out.rearrange("(g p u e) h -> g u p e h", p=P, u=2, e=2)
+    out0_hbm = out_0.rearrange("(g p u e) h -> g u p e h", p=P, u=2, e=2)
+    th_hbm = th.rearrange("(g p j) q -> g p j q", p=P, j=4)
+    h_hbm = h_enc2.rearrange("(g p j) h -> g p j h", p=P, j=4)
+    wd_hbm = Wd1.rearrange("(c p j) q -> c p j q", p=P, j=4)
+    we_hbm = We3.rearrange("(b t i) h -> i b t h", t=4, i=8)
 
     with ExitStack() as ctx:
         sb = ctx.enter_context(tc.tile_pool(name="sb", bufs=1))
         ps = ctx.enter_context(tc.psum_pool(name="ps", bufs=1))
         ctx.enter_context(tc.manual_schedule())
 
-        def sbt(tag, shape, dtype, bufs=1):
+        def sbuf(tag, shape, dtype, bufs=1):
             return sb.tile(shape, dtype, name=tag, tag=tag, bufs=bufs, align_bytes=64)
+
+        def staging(shape, dtype):
+            return sbuf("staging", shape, dtype, 5)
 
         free_banks = list(range(8))
 
-        def take_bank(dtype=F32):
-            n = free_banks[0]
-            free_banks.remove(n)
-            width = 512 if dtype == F32 else 1024
-            return n, ps.tile([P, width], dtype, name="bank%d" % n, tag="bank%d" % n, bufs=1)
+        def take_bank():
+            number = free_banks[0]
+            free_banks.remove(number)
+            return number, ps.tile([P, PASS], F32, name="bank%d" % number, tag="bank%d" % number, bufs=1)
 
-        def give_bank(n):
-            free_banks.append(n)
-
-        def copy(engine, out, in_):
-            if engine == "s":
-                act.copy(out=out, in_=in_)
-            else:
-                vec.tensor_copy(out=out, in_=in_)
-
-        def mx_tiles(tag, width, bufs):
-            return sbt(tag + "_codes", [P, width], U32, bufs), sbt(tag + "_scales", [P, width], U8, bufs)
-
-        def quantize(dst, cols, src, fmt):
-            vec.quantize_mx(out=dst[0][:, cols].bitcast(fmt), scales=dst[1][:, cols], in_=src)
-
-        def mm(bank, lhs, lcols, lfmt, rhs, rcols, rfmt, start, stop):
-            pe.matmul_mx(out=bank[:], lhsT=lhs[0][:, lcols].bitcast(lfmt), lhsT_scale=lhs[1][:, lcols],
-                         rhs=rhs[0][:, rcols].bitcast(rfmt), rhs_scale=rhs[1][:, rcols], start=start, stop=stop)
+        def give_bank(number):
+            free_banks.append(number)
 
         def cols(n, width):
             return slice(n * width, (n + 1) * width)
 
-        warm = sbt("warm", [P, 1], F32)
-        vec.memset(warm[:], 0.0)
-        warm2 = sbt("warm2", [P, 1], F32)
-        act.activation(out=warm2[:], in_=warm[:], func=ACT.Sin)
-        ident = sbt("ident", [P, P], F32)
+        def mx_tiles(tag, width, bufs):
+            return sbuf(tag + "_codes", [P, width], U32, bufs), sbuf(tag + "_scales", [P, width], U8, bufs)
+
+        def quantize(dst, window, src, fmt):
+            vec.quantize_mx(out=dst[0][:, window].bitcast(fmt), scales=dst[1][:, window], in_=src)
+
+        def mx_pass(bank, lhs, lhs_cols, lhs_fmt, rhs, rhs_cols, rhs_fmt, start, stop):
+            pe.matmul_mx(out=bank[:], lhsT=lhs[0][:, lhs_cols].bitcast(lhs_fmt), lhsT_scale=lhs[1][:, lhs_cols],
+                         rhs=rhs[0][:, rhs_cols].bitcast(rhs_fmt), rhs_scale=rhs[1][:, rhs_cols], start=start, stop=stop)
+
+        def interleave(copy, dst, src):
+            copy(out=dst.rearrange("p (c i t) -> p c t i", i=4, t=4), in_=src.rearrange("p t (c i) -> p c t i", i=4))
+
+        zero_in = sbuf("zero_in", [P, 1], F32)
+        vec.memset(zero_in[:], 0.0)
+        zero = sbuf("zero", [P, 1], F32)
+        act.activation(out=zero[:], in_=zero_in[:], func=ACT.Sin)
+        ident = sbuf("ident", [P, P], F32)
         make_identity(nc, ident[:])
-        ident_bf = sbt("ident_bf", [P, P], BF16)
+        ident_bf = sbuf("ident_bf", [P, P], BF16)
         make_identity(nc, ident_bf[:])
 
-        y_t, g_t, th_t, h_t = {}, {}, {}, {}
+        y2_sb, grad_sb, th_sb, h_sb = {}, {}, {}, {}
 
-        def load_yg(g, u):
-            y_t[g, u] = sbt("y", [P, 2, H2], F32, 3)
-            nc.sync.dma_start(out=y_t[g, u][:], in_=y_v[g, u])
-            g_t[g, u] = sbt("g", [P, 2, H2], BF16, 4)
-            nc.sync.dma_start(out=g_t[g, u][:], in_=g_v[g, u])
+        def load_grad(g, u):
+            y2_sb[g, u] = sbuf("y2", [P, 2, H2], F32, 3)
+            nc.sync.dma_start(out=y2_sb[g, u][:], in_=y2_hbm[g, u])
+            grad_sb[g, u] = sbuf("grad", [P, 2, H2], BF16, 4)
+            nc.sync.dma_start(out=grad_sb[g, u][:], in_=grad_hbm[g, u])
 
         def load_th(g):
-            th_t[g] = sbt("th", [P, 4, NQ], F32, 2)
-            nc.sync.dma_start(out=th_t[g][:], in_=th_v[g])
+            th_sb[g] = sbuf("th", [P, 4, NQ], F32, 2)
+            nc.sync.dma_start(out=th_sb[g][:], in_=th_hbm[g])
 
         def load_h(g):
-            h_t[g] = sbt("h", [P, 4, H2], BF16, 2)
-            nc.sync.dma_start(out=h_t[g][:], in_=h_v[g])
+            h_sb[g] = sbuf("h", [P, 4, H2], BF16, 2)
+            nc.sync.dma_start(out=h_sb[g][:], in_=h_hbm[g])
 
-        ang = sbt("ang", [P, 2, 12], BF16)
-        nc.sync.dma_start(out=ang[:], in_=Pang.rearrange("l (p s) a -> p l (s a)", s=4))
-        wd_raw = sbt("stage", [P, 2, 4, NQ], BF16, 5)
-        we_raw = sbt("stage", [P, 4, H2], BF16, 5)
-
-        def load_we(i):
-            nc.sync.dma_start(out=we_raw[i:P:8, :, :], in_=we_v[i])
-
-        nc.sync.dma_start(out=wd_raw[:, 0], in_=wd_v[0])
+        angles_raw = sbuf("angles_raw", [P, 2, 12], BF16)
+        nc.sync.dma_start(out=angles_raw[:], in_=gate_angles.rearrange("l (m s) a -> m l (s a)", s=4))
+        wd_raw = staging([P, 2, 4, NQ], BF16)
+        we_raw = staging([P, 4, H2], BF16)
+        nc.sync.dma_start(out=wd_raw[:, 0], in_=wd_hbm[0])
         load_th(0)
+        nc.sync.dma_start(out=wd_raw[:, 1], in_=wd_hbm[1])
         for i in range(8):
-            load_we(i)
-        load_yg(0, 0)
-        nc.sync.dma_start(out=wd_raw[:, 1], in_=wd_v[1])
-        load_yg(0, 1)
+            nc.sync.dma_start(out=we_raw[i:P:8, :, :], in_=we_hbm[i])
+        load_grad(0, 0)
+        load_grad(0, 1)
         load_th(1)
-        load_yg(1, 0)
+        load_grad(1, 0)
         load_h(0)
 
-        small_n = [0]
+        small_tags = []
 
         def small(shape, dtype=F32):
-            small_n.append(0)
-            return sbt("small%d" % len(small_n), [P] + shape, dtype)
+            small_tags.append("small%d" % len(small_tags))
+            return sbuf(small_tags[-1], [P] + shape, dtype)
 
-        steps = []
+        pick_row = sbuf("pick_row", [P, 4 * P], BF16)
+        vec.tensor_copy(out=pick_row[:].rearrange("m (t b a s) -> m t b a s", t=4, a=2, s=4),
+                        in_=ident_bf[:].rearrange("m (b t a) -> m t b a", t=4, a=2).unsqueeze(4).to_broadcast([P, 4, 16, 2, 4]))
+        pick_qubit = small([4])
+        vec.tensor_reduce(out=pick_qubit[:], in_=ident_bf[:].rearrange("p (m s) -> p s m", s=4), axis=mybir.AxisListType.X, op=ALU.add)
+        number, bank = take_bank()
+        for t in range(4):
+            pe.matmul(bank[:, cols(t, 24)], lhsT=pick_row[:, cols(t, P)], rhs=angles_raw[:].rearrange("m l x -> m (l x)"),
+                      start=True, stop=True)
+        masked = small([8, 4, 3])
+        vec.tensor_tensor(out=masked[:], in0=bank[:, 0:96].rearrange("p (x s a) -> p x s a", s=4, a=3),
+                          in1=pick_qubit[:].unsqueeze(1).unsqueeze(3).to_broadcast([P, 8, 4, 3]), op=ALU.mult)
+        give_bank(number)
+        angles_tile = small([8, 3])
+        vec.tensor_reduce(out=angles_tile[:], in_=masked[:].rearrange("p x s a -> p x a s"), axis=mybir.AxisListType.X, op=ALU.add)
+        angles = angles_tile[:].rearrange("p x a -> p (x a)")
 
-        def tt(a, b, op, shape, out=None):
-            res = small(shape)[:] if out is None else out
-            steps.append(lambda: vec.tensor_tensor(out=res, in0=a, in1=b, op=op))
+        queued = []
+
+        def tt(a, b, op, shape):
+            res = small(shape)[:]
+            queued.append(lambda: vec.tensor_tensor(out=res, in0=a, in1=b, op=op))
             return res
 
-        def ts(a, s1, s2, op0, op1, shape, dtype=F32, out=None):
-            res = small(shape, dtype)[:] if out is None else out
-            steps.append(lambda: vec.tensor_scalar(out=res, in0=a, scalar1=s1, scalar2=s2, op0=op0, op1=op1))
+        def ts(res, a, s1, s2, op0, op1):
+            queued.append(lambda: vec.tensor_scalar(out=res, in0=a, scalar1=s1, scalar2=s2, op0=op0, op1=op1))
             return res
 
-        def stt(a, s, b, op0, op1, shape, out=None):
-            res = small(shape)[:] if out is None else out
-            steps.append(lambda: vec.scalar_tensor_tensor(out=res, in0=a, scalar=s, in1=b, op0=op0, op1=op1))
+        def stt(res, a, s, b, op0, op1):
+            queued.append(lambda: vec.scalar_tensor_tensor(out=res, in0=a, scalar=s, in1=b, op0=op0, op1=op1))
             return res
 
-        def scal(out, a, func, scale, bias):
-            steps.append(lambda: act.activation(out=out, in_=a, func=func, scale=scale, bias=bias))
+        def scalar_fn(res, a, func, scale, bias):
+            queued.append(lambda: act.activation(out=res, in_=a, func=func, scale=scale, bias=bias))
 
         def recip(a):
             res = small([4])[:]
-            steps.append(lambda: vec.reciprocal(out=res, in_=a))
+            queued.append(lambda: vec.reciprocal(out=res, in_=a))
             return res
+
+        def column():
+            return small([4])[:]
 
         def both(a):
             return a.unsqueeze(1).to_broadcast([P, 2, 4])
 
-        pick_rows = sbt("pick_rows", [P, 512], BF16)
-        vec.tensor_copy(out=pick_rows[:].rearrange("p (t g a s) -> p t g a s", t=4, a=2, s=4),
-                        in_=ident_bf[:].rearrange("p (g t a) -> p t g a", t=4, a=2).unsqueeze(4).to_broadcast([P, 4, 16, 2, 4]))
-        pick_slot = small([4])
-        vec.tensor_reduce(out=pick_slot[:], in_=ident_bf[:].rearrange("p (m s) -> p s m", s=4), axis=mybir.AxisListType.X, op=ALU.add)
-        n, bank = take_bank()
-        for t in range(4):
-            pe.matmul(bank[:, cols(t, 24)], lhsT=pick_rows[:, cols(t, P)], rhs=ang[:].rearrange("p l x -> p (l x)"), start=True, stop=True)
-        picked = small([8, 4, 3])
-        vec.tensor_tensor(out=picked[:], in0=bank[:, 0:96].rearrange("p (x s a) -> p x s a", s=4, a=3),
-                          in1=pick_slot[:].unsqueeze(1).unsqueeze(3).to_broadcast([P, 8, 4, 3]), op=ALU.mult)
-        give_bank(n)
-        ang_own = small([8, 3])
-        vec.tensor_reduce(out=ang_own[:], in_=picked[:].rearrange("p x s a -> p x a s"), axis=mybir.AxisListType.X, op=ALU.add)
-        ang_flat = ang_own[:].rearrange("p x a -> p (x a)")
+        def issue(count):
+            for step in queued[:count]:
+                step()
+                queued.remove(step)
+
         turns = small([2, 24], I32)
-        ts(ang_flat, 1.0 / TWO_PI, -0.25, ALU.mult, ALU.add, None, out=turns[:, 0, :])
-        ts(ang_flat, 1.0 / TWO_PI, 0.0, ALU.mult, ALU.add, None, out=turns[:, 1, :])
-        red = stt(turns[:], -TWO_PI, ang_flat.unsqueeze(1).to_broadcast([P, 2, 24]), ALU.mult, ALU.add, [2, 24])
+        ts(turns[:, 0, :], angles, 1.0 / TWO_PI, -0.25, ALU.mult, ALU.add)
+        ts(turns[:, 1, :], angles, 1.0 / TWO_PI, 0.0, ALU.mult, ALU.add)
+        reduced = stt(small([2, 24])[:], turns[:], -TWO_PI, angles.unsqueeze(1).to_broadcast([P, 2, 24]), ALU.mult, ALU.add)
         trig = small([2, 24])
         folded = small([2, 24])
-        scal(folded[:, 0, :], red[:, 0, :], ACT.Abs, 1.0, -0.5 * math.pi)
-        scal(folded[:, 1, :], red[:, 1, :], ACT.Abs, 1.0, 0.0)
-        scal(trig[:], folded[:], ACT.Sin, -1.0, 0.5 * math.pi)
-        sc = trig[:].rearrange("p w (s l a) -> p l a w s", l=2, a=3)
-        w1 = tt(both(sc[:, 1, 1, 1]), sc[:, 1, 0], ALU.mult, [2, 4])
-        pa = tt(both(sc[:, 1, 1, 0]), sc[:, 0, 2], ALU.mult, [2, 4])
-        pb = tt(both(w1[:, 0]), sc[:, 0, 2], ALU.mult, [2, 4])
-        pc = tt(both(w1[:, 1]), sc[:, 0, 1], ALU.mult, [2, 4])
-        wx2 = tt(pb[:, 0], pa[:, 1], ALU.subtract, [4])
-        wy2 = tt(pb[:, 1], pa[:, 0], ALU.add, [4])
-        pd = tt(both(wx2), sc[:, 0, 1], ALU.mult, [2, 4])
-        pe_ = tt(wy2, sc[:, 0, 0, 0], ALU.mult, [4])
-        yx = small([2, 4])
-        wz3 = tt(pd[:, 0], pc[:, 1], ALU.add, [4])
-        sa = stt(pd[:, 1], 1e-30, pc[:, 0], ALU.add, ALU.subtract, [4])
-        pf = tt(wz3, sc[:, 0, 0, 1], ALU.mult, [4])
-        ca = tt(pf, pe_, ALU.subtract, [4])
-        stt(sa, TILT_TAN, ca, ALU.mult, ALU.add, None, out=yx[:, 0, :])
-        stt(ca, -TILT_TAN, sa, ALU.mult, ALU.add, None, out=yx[:, 1, :])
-        mag = stt(yx[:], -1.0, yx[:], ALU.mult, ALU.max, [2, 4])
-        side = ts(yx[:, 1, :], 0.0, GUESS, ALU.is_ge, ALU.mult, [4])
-        den = tt(mag[:, 0], mag[:, 1], ALU.add, [4])
-        num = stt(side, -0.5 * GUESS, yx[:, 0, :], ALU.add, ALU.mult, [4])
-        rden = recip(den)
-        guess = tt(num, rden, ALU.mult, [4])
-        sc0 = small([2, 4])
-        scal(sc0[:, 0, :], guess, ACT.Sin, 1.0, 0.0)
-        scal(sc0[:, 1, :], guess, ACT.Sin, 1.0, 0.5 * math.pi)
-        gy = tt(both(yx[:, 0, :]), sc0[:], ALU.mult, [2, 4])
-        gx = tt(both(yx[:, 1, :]), sc0[:], ALU.mult, [2, 4])
-        dn = tt(gy[:, 0], gx[:, 1], ALU.add, [4])
-        nn = tt(gy[:, 1], gx[:, 0], ALU.subtract, [4])
-        rdn = recip(dn)
-        tan = tt(nn, rdn, ALU.mult, [4])
-        sq = tt(tan, tan, ALU.mult, [4])
-        h1 = ts(sq, -1.0 / 7.0, 1.0 / 5.0, ALU.mult, ALU.add, [4])
-        g1 = ts(sq, TILT_COS / 16.0, -TILT_COS / 8.0, ALU.mult, ALU.add, [4])
-        h2 = tt(h1, sq, ALU.mult, [4])
-        g2 = tt(g1, sq, ALU.mult, [4])
-        h3 = stt(h2, -1.0 / 3.0, sq, ALU.add, ALU.mult, [4])
-        g3 = stt(g2, 0.5 * TILT_COS, sq, ALU.add, ALU.mult, [4])
-        err = stt(h3, 1.0, tan, ALU.add, ALU.mult, [4])
-        pr = small([2, 4])
-        stt(g3, TILT_COS, dn, ALU.add, ALU.mult, None, out=pr[:, 1, :])
-        stt(guess, -TILT, err, ALU.add, ALU.add, None, out=pr[:, 0, :])
+        scalar_fn(folded[:, 0, :], reduced[:, 0, :], ACT.Abs, 1.0, -0.5 * math.pi)
+        scalar_fn(folded[:, 1, :], reduced[:, 1, :], ACT.Abs, 1.0, zero[:])
+        scalar_fn(trig[:], folded[:], ACT.Sin, -1.0, 0.5 * math.pi)
+        trig_steps = len(queued)
 
-        def run_steps(n):
-            for step in steps[:n]:
-                step()
-            for step in steps[:n]:
-                steps.remove(step)
+        sin_cos = trig[:].rearrange("p w (t l a) -> p l a w t", l=2, a=3)
+        rx0, ry0, rz0, rx1, ry1 = sin_cos[:, 0, 0], sin_cos[:, 0, 1], sin_cos[:, 0, 2], sin_cos[:, 1, 0], sin_cos[:, 1, 1]
+        yz_rx1 = tt(both(ry1[:, 1]), rx1, ALU.mult, [2, 4])
+        x_rz = tt(both(ry1[:, 0]), rz0, ALU.mult, [2, 4])
+        y_rz = tt(both(yz_rx1[:, 0]), rz0, ALU.mult, [2, 4])
+        z_ry = tt(both(yz_rx1[:, 1]), ry0, ALU.mult, [2, 4])
+        x_after_rz = tt(y_rz[:, 0], x_rz[:, 1], ALU.subtract, [4])
+        y_after_rz = tt(y_rz[:, 1], x_rz[:, 0], ALU.add, [4])
+        x_ry = tt(both(x_after_rz), ry0, ALU.mult, [2, 4])
+        y_rx = tt(y_after_rz, rx0[:, 0], ALU.mult, [4])
+        z_after_ry = tt(x_ry[:, 0], z_ry[:, 1], ALU.add, [4])
+        sa = stt(column(), x_ry[:, 1], TINY, z_ry[:, 0], ALU.add, ALU.subtract)
+        z_rx = tt(z_after_ry, rx0[:, 1], ALU.mult, [4])
+        ca = tt(z_rx, y_rx, ALU.subtract, [4])
 
-        wd_mx = [mx_tiles("wd%d" % c, 512, 1) for c in range(2)]
-        we_mx = mx_tiles("we", 1024, 1)
-        wd_grp, we_grp = {}, {}
+        tilted = small([2, 4])
+        tilted_y = stt(tilted[:, 0, :], sa, TILT_TAN, ca, ALU.mult, ALU.add)
+        tilted_x = stt(tilted[:, 1, :], ca, -TILT_TAN, sa, ALU.mult, ALU.add)
+        magnitude = stt(small([2, 4])[:], tilted[:], -1.0, tilted[:], ALU.mult, ALU.max)
+        side = ts(column(), tilted_x, 0.0, GUESS_SPAN, ALU.is_ge, ALU.mult)
+        norm = tt(magnitude[:, 0], magnitude[:, 1], ALU.add, [4])
+        signed_y = stt(column(), side, -0.5 * GUESS_SPAN, tilted_y, ALU.add, ALU.mult)
+        guess = tt(signed_y, recip(norm), ALU.mult, [4])
+        guess_trig = small([2, 4])
+        scalar_fn(guess_trig[:, 0, :], guess, ACT.Sin, 1.0, 0.0)
+        scalar_fn(guess_trig[:, 1, :], guess, ACT.Sin, 1.0, 0.5 * math.pi)
+        guess_steps = len(queued) - trig_steps
 
-        def wd_interleave(c, engine):
-            wd_grp[c] = sbt("ag" if c == 0 else "bg", [P, 2048], BF16)
-            copy(engine, wd_grp[c][:].rearrange("p (t g i j) -> p t g i j", t=4, i=8, j=4),
-                 wd_raw[:, c].rearrange("p j (g t i) -> p t g i j", t=4, i=8))
+        y_guess = tt(both(tilted_y), guess_trig[:], ALU.mult, [2, 4])
+        x_guess = tt(both(tilted_x), guess_trig[:], ALU.mult, [2, 4])
+        along = tt(y_guess[:, 0], x_guess[:, 1], ALU.add, [4])
+        across = tt(y_guess[:, 1], x_guess[:, 0], ALU.subtract, [4])
+        tangent = tt(across, recip(along), ALU.mult, [4])
+        tan_sq = tt(tangent, tangent, ALU.mult, [4])
+        atan_1 = ts(column(), tan_sq, -1.0 / 7.0, 1.0 / 5.0, ALU.mult, ALU.add)
+        root_1 = ts(column(), tan_sq, TILT_COS / 16.0, -TILT_COS / 8.0, ALU.mult, ALU.add)
+        atan_2 = tt(atan_1, tan_sq, ALU.mult, [4])
+        root_2 = tt(root_1, tan_sq, ALU.mult, [4])
+        atan_3 = stt(column(), atan_2, -1.0 / 3.0, tan_sq, ALU.add, ALU.mult)
+        root_3 = stt(column(), root_2, 0.5 * TILT_COS, tan_sq, ALU.add, ALU.mult)
+        err = stt(column(), atan_3, 1.0, tangent, ALU.add, ALU.mult)
+        phase_amp = small([2, 4])
+        amp = stt(phase_amp[:, 1, :], root_3, TILT_COS, along, ALU.add, ALU.mult)
+        phase = stt(phase_amp[:, 0, :], guess, -TILT, err, ALU.add, ALU.add)
+
+        wd_mx = [mx_tiles("wd%d" % c, PASS, 1) for c in range(2)]
+        we_mx = mx_tiles("we", H2, 1)
+        wd_words, we_words = {}, {}
+
+        def wd_interleave(c):
+            wd_words[c] = sbuf(("qubit_words", "token_words")[c], [P, 4 * PASS], BF16)
+            act.copy(out=wd_words[c][:].rearrange("p (t b i j) -> p t b i j", t=4, i=8, j=4),
+                     in_=wd_raw[:, c].rearrange("p j (b t i) -> p t b i j", t=4, i=8))
 
         def wd_quantize(c):
-            quantize(wd_mx[c], cols(0, 512), wd_grp[c][:], E4)
-
-        def interleave(engine, dst, src):
-            copy(engine, dst.rearrange("p (c i t) -> p c t i", i=4, t=4), src.rearrange("p t (c i) -> p c t i", i=4))
+            quantize(wd_mx[c], cols(0, PASS), wd_words[c][:], E4)
 
         def we_interleave(n):
-            we_grp[n] = sbt("hg", [P, 2048], BF16, 2)
-            interleave("s", we_grp[n][:], we_raw[:, :, cols(n, 512)])
+            we_words[n] = sbuf("h_words", [P, 4 * PASS], BF16, 2)
+            interleave(on_scalar, we_words[n][:], we_raw[:, :, cols(n, PASS)])
 
         def we_quantize(n):
-            quantize(we_mx, cols(n, 512), we_grp[n][:], E4)
+            quantize(we_mx, cols(n, PASS), we_words[n][:], E4)
 
-        dz2_t, dzg, dz2_mx = {}, {}, {}
+        dz2_sb, dz2_words, dz2_mx = {}, {}, {}
 
         def mask(g, u):
-            dz2_t[g, u] = sbt("dz2", [P, 2 * H2], BF16, 2)
-            vec.scalar_tensor_tensor(out=dz2_t[g, u][:], in0=y_t[g, u][:].rearrange("p e h -> p (e h)"), scalar=0.0,
-                                     in1=g_t[g, u][:].rearrange("p e h -> p (e h)"), op0=ALU.is_gt, op1=ALU.mult)
+            dz2_sb[g, u] = sbuf("dz2", [P, 2 * H2], BF16, 2)
+            vec.scalar_tensor_tensor(out=dz2_sb[g, u][:], in0=y2_sb[g, u][:].rearrange("p e h -> p (e h)"), scalar=0.0,
+                                     in1=grad_sb[g, u][:].rearrange("p e h -> p (e h)"), op0=ALU.is_gt, op1=ALU.mult)
 
         def turn_dz2(g, u):
-            words = dz2_t[g, u][:].bitcast(F32)
+            pairs = dz2_sb[g, u][:].bitcast(F32)
             for c in range(2):
                 if u == 0:
-                    dzg[g, c] = sbt("dzg", [P, 2048], BF16, 2)
-                n, bank = take_bank()
+                    dz2_words[g, c] = sbuf("dz2_words", [P, 4 * PASS], BF16, 2)
+                number, bank = take_bank()
                 for e in range(2):
                     for f in range(2):
-                        first = 512 * e + 256 * c + f
-                        pe.transpose(bank[:, cols(2 * e + f, P)], words[:, first:512 * e + 256 * (c + 1):2], ident[:])
-                act.copy(out=dzg[g, c][:].bitcast(F32)[:, cols(u, 512)].rearrange("p (m e f) -> p m e f", e=2, f=2),
-                         in_=bank[:].rearrange("p (e f m) -> p m e f", e=2, f=2))
-                give_bank(n)
+                        first = 512 * e + 256 * c
+                        pe.transpose(bank[:, cols(2 * e + f, P)], pairs[:, first + f:first + 256:2], ident[:])
+                act.copy(out=dz2_words[g, c][:].bitcast(F32)[:, cols(u, PASS)].rearrange("m (p e f) -> m p e f", e=2, f=2),
+                         in_=bank[:].rearrange("m (e f p) -> m p e f", e=2, f=2))
+                give_bank(number)
 
-        def quant_dz2(g, c):
-            dz2_mx[g, c] = mx_tiles("dz2", 512, 2)
-            quantize(dz2_mx[g, c], cols(0, 512), dzg[g, c][:], E5)
-
-        k_t, r_t, ab_t, s_t, dh_t, dz1_t = {}, {}, {}, {}, {}, {}
-
-        def count_turns(g, js=slice(0, 4)):
-            if js.start == 0:
-                k_t[g] = sbt("k", [P, 4, NQ], I32)
-            vec.tensor_scalar(out=k_t[g][:, js], in0=th_t[g][:, js], scalar1=1.0 / TWO_PI, scalar2=-TILT / TWO_PI, op0=ALU.mult, op1=ALU.add)
-
-        def reduce_angle(g, t, xs=slice(0, 64)):
-            if xs.start == 0:
-                r_t[g, t] = sbt("r", [P, NQ], F32, 4)
-            pick = "p j (g t i) -> p t (j g) i"
-            vec.scalar_tensor_tensor(out=r_t[g, t][:].rearrange("p (x i) -> p x i", i=8)[:, xs],
-                                     in0=k_t[g][:].rearrange(pick, t=4, i=8)[:, t, xs], scalar=-TWO_PI,
-                                     in1=th_t[g][:].rearrange(pick, t=4, i=8)[:, t, xs], op0=ALU.mult, op1=ALU.add)
-
-        def sine(g, t):
-            n, bank = take_bank()
-            for j in range(4):
-                pe.transpose(bank[:, cols(j, P)], r_t[g, t][:, cols(j, P)], ident[:])
-            tp, x = divmod(t, 2)
-            if x == 0:
-                ab_t[g, tp] = sbt("ab", [P, 1024], F32)
-            act.activation(out=ab_t[g, tp][:, cols(x, 512)].rearrange("p (u m e) -> p u m e", u=2, e=2),
-                           in_=bank[:].rearrange("p (u e m) -> p u m e", u=2, e=2), func=ACT.Abs, bias=pr[:, 0, t:t + 1])
-            give_bank(n)
-            if x == 1:
-                s_t[g, tp] = sbt("s", [P, 1024], F32, 2)
-                act.activation(out=s_t[g, tp][:], in_=ab_t[g, tp][:], func=ACT.Sin, scale=-1.0, bias=0.5 * math.pi)
-
-        def dh_mm(g, t):
-            dh_t[g, t] = take_bank()
+        def dz2_quantize(g):
             for c in range(2):
-                mm(dh_t[g, t][1], wd_mx[c], cols(t, P), E4, dz2_mx[g, c], cols(0, 512), E5, c == 0, c == 1)
+                dz2_mx[g, c] = mx_tiles("dz2", PASS, 2)
+                quantize(dz2_mx[g, c], cols(0, PASS), dz2_words[g, c][:], E5)
 
-        def make_dz1(g, t):
-            if t == 0:
-                dz1_t[g] = sbt("dz1", [P, 2048], BF16)
-            n, bank = dh_t[g, t]
-            vec.scalar_tensor_tensor(out=dz1_t[g][:, cols(t, 512)], in0=bank[:], scalar=pr[:, 1, t:t + 1],
-                                     in1=s_t[g, t // 2][:, cols(t % 2, 512)], op0=ALU.mult, op1=ALU.mult)
-            give_bank(n)
+        turns_sb, reduced_sb, folded_sb, cos_sb, dh_banks, dz1_sb = {}, {}, {}, {}, {}, {}
 
-        hg, h_mx, ag, bg, a_mx, b_mx = {}, {}, {}, {}, {}, {}
+        def count_turns(g, places=slice(0, 4)):
+            if places.start == 0:
+                turns_sb[g] = sbuf("turns", [P, 4, NQ], I32)
+            vec.tensor_scalar(out=turns_sb[g][:, places], in0=th_sb[g][:, places], scalar1=1.0 / TWO_PI, scalar2=-TILT / TWO_PI,
+                              op0=ALU.mult, op1=ALU.add)
 
-        def h_interleave(g, x, engine):
-            n, z = divmod(x, 2)
-            if z == 0:
-                hg[g, n] = sbt("hg", [P, 2048], BF16, 2)
-            interleave(engine, hg[g, n][:, cols(z, 1024)], h_t[g][:, :, cols(x, 256)])
+        def reduce_angle(g, t, runs=slice(0, 64)):
+            if runs.start == 0:
+                reduced_sb[g, t] = sbuf("reduced", [P, NQ], F32, 4)
+            pick = "p j (b t i) -> p t (j b) i"
+            vec.scalar_tensor_tensor(out=reduced_sb[g, t][:].rearrange("p (x i) -> p x i", i=8)[:, runs],
+                                     in0=turns_sb[g][:].rearrange(pick, t=4, i=8)[:, t, runs], scalar=-TWO_PI,
+                                     in1=th_sb[g][:].rearrange(pick, t=4, i=8)[:, t, runs], op0=ALU.mult, op1=ALU.add)
 
-        def h_quantize(g, n):
-            if n == 0:
-                h_mx[g] = mx_tiles("h", 1024, 4)
-            quantize(h_mx[g], cols(n, 512), hg[g, n][:], E4)
+        def cosine(g, pair):
+            folded_sb[g, pair] = sbuf("folded", [P, 2 * PASS], F32)
+            for x in range(2):
+                t = 2 * pair + x
+                number, bank = take_bank()
+                for j in range(4):
+                    pe.transpose(bank[:, cols(j, P)], reduced_sb[g, t][:, cols(j, P)], ident[:])
+                act.activation(out=folded_sb[g, pair][:, cols(x, PASS)].rearrange("q (u p e) -> q u p e", u=2, e=2),
+                               in_=bank[:].rearrange("q (u e p) -> q u p e", u=2, e=2), func=ACT.Abs, bias=phase[:, t:t + 1])
+                give_bank(number)
+            cos_sb[g, pair] = sbuf("cos", [P, 2 * PASS], F32, 2)
+            act.activation(out=cos_sb[g, pair][:], in_=folded_sb[g, pair][:], func=ACT.Sin, scale=-1.0, bias=0.5 * math.pi)
 
-        def a_interleave(g, us):
-            if us.start == 0:
-                ag[g] = sbt("ag", [P, 2048], BF16)
-            dst = ag[g][:].rearrange("p (u e m t) -> p u e m t", u=2, e=2, t=4)
-            src = dz1_t[g][:].rearrange("p (t u m e) -> p u e m t", t=4, u=2, e=2)
-            vec.tensor_copy(out=dst[:, us], in_=src[:, us])
+        def dh_matmul(g, pair):
+            for t in (2 * pair, 2 * pair + 1):
+                dh_banks[g, t] = take_bank()
+                for c in range(2):
+                    mx_pass(dh_banks[g, t][1], wd_mx[c], cols(t, P), E4, dz2_mx[g, c], cols(0, PASS), E5, c == 0, c == 1)
 
-        def b_turn(g, tp, engine):
-            if tp == 0:
-                bg[g] = sbt("bg", [P, 2048], BF16)
-            words = dz1_t[g][:].bitcast(F32)
-            n, bank = take_bank()
+        def make_dz1(g, pair):
+            if pair == 0:
+                dz1_sb[g] = sbuf("dz1", [P, 4 * PASS], BF16)
+            for x in range(2):
+                t = 2 * pair + x
+                number, bank = dh_banks[g, t]
+                vec.scalar_tensor_tensor(out=dz1_sb[g][:, cols(t, PASS)], in0=bank[:], scalar=amp[:, t:t + 1],
+                                         in1=cos_sb[g, pair][:, cols(x, PASS)], op0=ALU.mult, op1=ALU.mult)
+                give_bank(number)
+
+        h_words, h_mx, qubit_words, token_words, dz1_qubit_mx, dz1_token_mx = {}, {}, {}, {}, {}, {}
+
+        def h_interleave(g, quarter, copy):
+            n, x = divmod(quarter, 2)
+            if x == 0:
+                h_words[g, n] = sbuf("h_words", [P, 4 * PASS], BF16, 2)
+            interleave(copy, h_words[g, n][:, cols(x, 1024)], h_sb[g][:, :, cols(quarter, 256)])
+
+        def h_quantize(g):
+            h_mx[g] = mx_tiles("h", H2, GROUPS)
+            for n in range(2):
+                quantize(h_mx[g], cols(n, PASS), h_words[g, n][:], E4)
+
+        def dz1_interleave(g, halves):
+            if halves.start == 0:
+                qubit_words[g] = sbuf("qubit_words", [P, 4 * PASS], BF16)
+            dst = qubit_words[g][:].rearrange("q (u e p t) -> q u e p t", u=2, e=2, t=4)
+            src = dz1_sb[g][:].rearrange("q (t u p e) -> q u e p t", t=4, u=2, e=2)
+            vec.tensor_copy(out=dst[:, halves], in_=src[:, halves])
+
+        def dz1_qubit_quantize(g, halves):
+            if halves.start == 0:
+                dz1_qubit_mx[g] = mx_tiles("dz1_qubit", PASS, 1)
+            quantize(dz1_qubit_mx[g], slice(256 * halves.start, 256 * halves.stop),
+                     qubit_words[g][:, 1024 * halves.start:1024 * halves.stop], E5)
+
+        def turn_dz1(g, pair):
+            if pair == 0:
+                token_words[g] = sbuf("token_words", [P, 4 * PASS], BF16)
+            pairs = dz1_sb[g][:].bitcast(F32)
+            number, bank = take_bank()
             for x in range(4):
-                pe.transpose(bank[:, cols(x, P)], words[:, cols(4 * tp + x, P)], ident[:])
-            dst = bg[g][:].bitcast(F32).rearrange("p (g t i u) -> p g t i u", t=4, i=8, u=2)
-            copy(engine, dst[:, :, 2 * tp:2 * tp + 2], bank[:].rearrange("p (t u g i) -> p g t i u", t=2, u=2, i=8))
-            give_bank(n)
+                pe.transpose(bank[:, cols(x, P)], pairs[:, cols(4 * pair + x, P)], ident[:])
+            dst = token_words[g][:].bitcast(F32).rearrange("p (b t i u) -> p b t i u", t=4, i=8, u=2)
+            act.copy(out=dst[:, :, 2 * pair:2 * pair + 2], in_=bank[:].rearrange("p (t u b i) -> p b t i u", t=2, u=2, i=8))
+            give_bank(number)
 
-        def a_quantize(g, us):
-            if us.start == 0:
-                a_mx[g] = mx_tiles("a", 512, 1)
-            quantize(a_mx[g], slice(256 * us.start, 256 * us.stop), ag[g][:, 1024 * us.start:1024 * us.stop], E5)
+        def dz1_token_quantize(g):
+            dz1_token_mx[g] = mx_tiles("dz1_token", PASS, GROUPS)
+            quantize(dz1_token_mx[g], cols(0, PASS), token_words[g][:], E5)
 
-        def b_quantize(g):
-            b_mx[g] = mx_tiles("b", 512, 4)
-            quantize(b_mx[g], cols(0, 512), bg[g][:], E5)
+        out0_sb, out1_banks = {}, {}
 
-        o_t = {}
-
-        def out0_tile(g, x, engine):
-            j, n = divmod(x, 2)
+        def out0_rows(g, j, copies):
             u, e = divmod(j, 2)
-            if e == 0 and n == 0:
-                o_t[g, u] = sbt("stage", [P, 2, H2], F32, 5)
-            b, bank = take_bank()
-            mm(bank, a_mx[g], cols(j, P), E5, we_mx, cols(n, 512), E4, True, True)
-            copy(engine, o_t[g, u][:, e, cols(n, 512)], bank[:])
-            give_bank(b)
-            if g == GROUPS - 1 and n == 1:
-                nc.sync.dma_start(out=o0_v[g, u][:, e], in_=o_t[g, u][:, e])
-            elif e == 1 and n == 1:
-                nc.sync.dma_start(out=o0_v[g, u], in_=o_t[g, u][:])
-
-        o1_banks = {}
-
-        def out1_open(qt):
+            if e == 0:
+                out0_sb[g, u] = staging([P, 2, H2], F32)
             for n in range(2):
-                o1_banks[qt, n] = take_bank()
-                for g in range(GROUPS - 1):
-                    mm(o1_banks[qt, n][1], b_mx[g], cols(qt, P), E5, h_mx[g], cols(n, 512), E4, g == 0, False)
+                number, bank = take_bank()
+                mx_pass(bank, dz1_qubit_mx[g], cols(j, P), E5, we_mx, cols(n, PASS), E4, True, True)
+                copies[n](out=out0_sb[g, u][:, e, cols(n, PASS)], in_=bank[:])
+                give_bank(number)
+            if g == LAST:
+                nc.sync.dma_start(out=out0_hbm[g, u][:, e], in_=out0_sb[g, u][:, e])
+            elif e == 1:
+                nc.sync.dma_start(out=out0_hbm[g, u], in_=out0_sb[g, u][:])
 
-        def out1_close(qt):
-            g = GROUPS - 1
-            res = sbt("stage", [P, H2], F32, 5)
+        def out1_open(rows):
             for n in range(2):
-                b, bank = o1_banks[qt, n]
-                mm(bank, b_mx[g], cols(qt, P), E5, h_mx[g], cols(n, 512), E4, False, True)
-                copy("sv"[n], res[:, cols(n, 512)], bank[:])
-                give_bank(b)
-            nc.sync.dma_start(out=out_1[cols(qt, P), :], in_=res[:])
+                out1_banks[rows, n] = take_bank()
+                for g in range(LAST):
+                    mx_pass(out1_banks[rows, n][1], dz1_token_mx[g], cols(rows, P), E5, h_mx[g], cols(n, PASS), E4, g == 0, False)
 
+        def out1_close(rows):
+            res = staging([P, H2], F32)
+            for n in range(2):
+                number, bank = out1_banks[rows, n]
+                mx_pass(bank, dz1_token_mx[LAST], cols(rows, P), E5, h_mx[LAST], cols(n, PASS), E4, False, True)
+                scalar_and_vector[n](out=res[:, cols(n, PASS)], in_=bank[:])
+                give_bank(number)
+            nc.sync.dma_start(out=out_1[cols(rows, P), :], in_=res[:])
+
+        scalar_only, vector_only, scalar_and_vector = (on_scalar, on_scalar), (on_vector, on_vector), (on_scalar, on_vector)
         both_halves = slice(0, 2)
-        run_steps(6)
-        wd_interleave(0, "s")
-        run_steps(9)
+
+        issue(trig_steps)
+        wd_interleave(0)
+        wd_interleave(1)
+        issue(LEAD)
         for j in range(4):
             count_turns(0, slice(j, j + 1))
-            run_steps(2)
+            issue(WEAVE)
         wd_quantize(0)
-        run_steps(5)
+        issue(guess_steps - LEAD - 4 * WEAVE)
         we_interleave(0)
         we_interleave(1)
         for t in range(4):
             for x in range(2):
-                reduce_angle(0, t, slice(32 * x, 32 * x + 32))
-                run_steps(2)
-        run_steps(len(steps))
+                reduce_angle(0, t, cols(x, 32))
+                issue(WEAVE)
+        issue(len(queued))
+
         mask(0, 0)
-        load_yg(1, 1)
+        load_grad(1, 1)
         load_h(1)
-        wd_interleave(1, "s")
+        cosine(0, 0)
         turn_dz2(0, 0)
-        sine(0, 0)
-        sine(0, 1)
-        we_quantize(0)
         mask(0, 1)
-        load_yg(2, 0)
+        load_grad(2, 0)
+        cosine(0, 1)
         turn_dz2(0, 1)
-        sine(0, 2)
-        sine(0, 3)
-        we_quantize(1)
         wd_quantize(1)
+        we_quantize(0)
+        we_quantize(1)
         count_turns(1)
-        quant_dz2(0, 0)
-        quant_dz2(0, 1)
         for t in range(4):
-            dh_mm(0, t)
+            reduce_angle(1, t)
+        dz2_quantize(0)
+        dh_matmul(0, 0)
+        dh_matmul(0, 1)
         mask(1, 0)
-        for x in range(3):
-            h_interleave(0, x, "s")
-        h_interleave(0, 3, "v")
+        for quarter in range(4):
+            h_interleave(0, quarter, on_scalar)
         load_h(2)
         load_th(2)
-        load_yg(2, 1)
-        for t in range(4):
-            make_dz1(0, t)
+        load_grad(2, 1)
+        make_dz1(0, 0)
         turn_dz2(1, 0)
+        make_dz1(0, 1)
+        cosine(1, 0)
+        mask(1, 1)
+        load_grad(3, 0)
+        h_quantize(0)
 
-        for i in range(1, GROUPS):
-            last = i == GROUPS - 1
-            for t in range(4):
-                reduce_angle(i, t)
-            if i == 1:
-                sine(i, 0)
-                sine(i, 1)
-                h_quantize(0, 0)
-                h_quantize(0, 1)
-                mask(1, 1)
-                load_yg(3, 0)
-                b_turn(i - 1, 0, "s")
-                b_turn(i - 1, 1, "s")
-                h_interleave(1, 0, "s")
-                turn_dz2(i, 1)
-                h_interleave(1, 1, "s")
-                h_interleave(1, 2, "v")
-                h_interleave(1, 3, "v")
+        for g in range(1, GROUPS):
+            if g == 1:
+                turn_dz1(0, 0)
+                turn_dz1(0, 1)
+                turn_dz2(1, 1)
+                dz1_interleave(0, both_halves)
+                for quarter in range(4):
+                    h_interleave(1, quarter, scalar_and_vector[quarter // 2])
                 load_h(3)
                 load_th(3)
-                a_interleave(i - 1, both_halves)
-                b_quantize(i - 1)
             else:
-                turn_dz2(i, 1)
-                sine(i, 0)
-                sine(i, 1)
-                a_interleave(i - 1, both_halves)
-                b_turn(i - 1, 0, "s")
-                b_turn(i - 1, 1, "s")
-            sine(i, 2)
-            sine(i, 3)
-            quant_dz2(i, 0)
-            quant_dz2(i, 1)
-            a_quantize(i - 1, both_halves)
-            dh_mm(i, 0)
-            dh_mm(i, 1)
-            if last:
+                for t in range(4):
+                    reduce_angle(g, t)
+                turn_dz2(g, 1)
+                cosine(g, 0)
+                dz1_interleave(g - 1, both_halves)
+                turn_dz1(g - 1, 0)
+                turn_dz1(g - 1, 1)
+            cosine(g, 1)
+            dz1_qubit_quantize(g - 1, both_halves)
+            dz2_quantize(g)
+            if g == LAST:
                 break
-            for x in range(4):
-                out0_tile(i - 1, x, "s")
-            h_quantize(i, 0)
-            h_quantize(i, 1)
-            if i > 1:
-                b_quantize(i - 1)
-            h_interleave(i + 1, 0, "s")
-            h_interleave(i + 1, 1, "s")
-            mask(i + 1, 0)
-            if i == 1:
-                load_yg(3, 1)
-            make_dz1(i, 0)
-            make_dz1(i, 1)
-            turn_dz2(i + 1, 0)
-            dh_mm(i, 2)
-            dh_mm(i, 3)
-            count_turns(i + 1)
-            for x in range(4, 8):
-                out0_tile(i - 1, x, "s")
-            h_interleave(i + 1, 2, "v" if i == 2 else "s")
-            h_interleave(i + 1, 3, "v")
-            mask(i + 1, 1)
-            make_dz1(i, 2)
-            make_dz1(i, 3)
+            dh_matmul(g, 0)
+            out0_rows(g - 1, 0, scalar_only)
+            out0_rows(g - 1, 1, scalar_only)
+            mask(g + 1, 0)
+            if g + 2 == LAST:
+                load_grad(LAST, 1)
+            h_quantize(g)
+            dz1_token_quantize(g - 1)
+            h_interleave(g + 1, 0, on_scalar)
+            make_dz1(g, 0)
+            turn_dz2(g + 1, 0)
+            h_interleave(g + 1, 1, on_scalar)
+            dh_matmul(g, 1)
+            count_turns(g + 1)
+            out0_rows(g - 1, 2, scalar_only)
+            out0_rows(g - 1, 3, scalar_only)
+            h_interleave(g + 1, 2, on_vector)
+            h_interleave(g + 1, 3, on_vector)
+            mask(g + 1, 1)
+            make_dz1(g, 1)
 
-        g = GROUPS - 1
-        h_quantize(g, 0)
-        h_quantize(g, 1)
-        b_quantize(g - 1)
-        for x in range(4):
-            out0_tile(g - 1, x, "v")
-        out0_tile(g - 1, 4, "s")
-        out0_tile(g - 1, 5, "s")
+        out0_rows(LAST - 1, 0, vector_only)
+        dh_matmul(LAST, 0)
+        h_quantize(LAST)
+        dz1_token_quantize(LAST - 1)
+        out0_rows(LAST - 1, 1, scalar_only)
+        dh_matmul(LAST, 1)
+        out0_rows(LAST - 1, 2, scalar_only)
+        make_dz1(LAST, 0)
+        out0_rows(LAST - 1, 3, scalar_only)
         out1_open(0)
-        out0_tile(g - 1, 6, "s")
-        out0_tile(g - 1, 7, "s")
-        dh_mm(g, 2)
-        dh_mm(g, 3)
-        make_dz1(g, 0)
-        make_dz1(g, 1)
-        b_turn(g, 0, "s")
-        make_dz1(g, 2)
-        make_dz1(g, 3)
-        b_turn(g, 1, "s")
+        turn_dz1(LAST, 0)
+        make_dz1(LAST, 1)
+        turn_dz1(LAST, 1)
+
         out1_open(1)
-        a_interleave(g, slice(0, 1))
-        a_quantize(g, slice(0, 1))
-        a_interleave(g, slice(1, 2))
-        b_quantize(g)
-        for x in range(4):
-            out0_tile(g, x, "s")
-        a_quantize(g, slice(1, 2))
+        for u in range(2):
+            dz1_interleave(LAST, slice(u, u + 1))
+        for u in range(2):
+            dz1_qubit_quantize(LAST, slice(u, u + 1))
+        dz1_token_quantize(LAST)
+        out0_rows(LAST, 0, scalar_and_vector)
+        out0_rows(LAST, 1, scalar_and_vector)
         out1_close(0)
         out1_close(1)
-        for x in range(4, 8):
-            out0_tile(g, x, "sv"[x % 2])
         out1_open(2)
+        out0_rows(LAST, 2, scalar_and_vector)
+        out0_rows(LAST, 3, scalar_and_vector)
         out1_close(2)
         out1_open(3)
         out1_close(3)

@@ -45,7 +45,7 @@ def tile_unifiedautoencodernet_pa_v_kernel(tc, h_enc2, We3, be3, gate_angles, Wd
     th_hbm = th.rearrange("(g p j) q -> g p j q", p=P, j=4)
     h_hbm = h_enc2.rearrange("(g p j) h -> g p j h", p=P, j=4)
     wd_hbm = Wd1.rearrange("(c p j) q -> c p j q", p=P, j=4)
-    we_hbm = We3.rearrange("(b t i) h -> i b t h", t=4, i=8)
+    we_hbm = We3.rearrange("(r t i) h -> i r t h", t=4, i=4)
 
     with ExitStack() as ctx:
         sb = ctx.enter_context(tc.tile_pool(name="sb", bufs=1))
@@ -116,8 +116,8 @@ def tile_unifiedautoencodernet_pa_v_kernel(tc, h_enc2, We3, be3, gate_angles, Wd
         nc.sync.dma_start(out=wd_raw[:, 0], in_=wd_hbm[0])
         load_th(0)
         nc.sync.dma_start(out=wd_raw[:, 1], in_=wd_hbm[1])
-        for i in range(8):
-            nc.sync.dma_start(out=we_raw[i:P:8, :, :], in_=we_hbm[i])
+        for i in range(4):
+            nc.sync.dma_start(out=we_raw[i:P:4, :, :], in_=we_hbm[i])
         load_grad(0, 0)
         load_grad(0, 1)
         load_th(1)
@@ -131,8 +131,8 @@ def tile_unifiedautoencodernet_pa_v_kernel(tc, h_enc2, We3, be3, gate_angles, Wd
             return sbuf(small_tags[-1], [P] + shape, dtype)
 
         pick_row = sbuf("pick_row", [P, 4 * P], BF16)
-        vec.tensor_copy(out=pick_row[:].rearrange("m (t b a s) -> m t b a s", t=4, a=2, s=4),
-                        in_=ident_bf[:].rearrange("m (b t a) -> m t b a", t=4, a=2).unsqueeze(4).to_broadcast([P, 4, 16, 2, 4]))
+        vec.tensor_copy(out=pick_row[:].rearrange("m (t r i) -> m t r i", t=4, i=4),
+                        in_=ident_bf[:].rearrange("m (r t) -> m t r", t=4).unsqueeze(3).to_broadcast([P, 4, 32, 4]))
         pick_qubit = small([4])
         vec.tensor_reduce(out=pick_qubit[:], in_=ident_bf[:].rearrange("p (m s) -> p s m", s=4), axis=mybir.AxisListType.X, op=ALU.add)
         number, bank = take_bank()
@@ -243,8 +243,8 @@ def tile_unifiedautoencodernet_pa_v_kernel(tc, h_enc2, We3, be3, gate_angles, Wd
 
         def wd_interleave(c):
             wd_words[c] = sbuf(("qubit_words", "token_words")[c], [P, 4 * PASS], BF16)
-            act.copy(out=wd_words[c][:].rearrange("p (t b i j) -> p t b i j", t=4, i=8, j=4),
-                     in_=wd_raw[:, c].rearrange("p j (b t i) -> p t b i j", t=4, i=8))
+            act.copy(out=wd_words[c][:].rearrange("p (t r i j) -> p t r i j", t=4, i=4, j=4),
+                     in_=wd_raw[:, c].rearrange("p j (r t i) -> p t r i j", t=4, i=4))
 
         def wd_quantize(c):
             quantize(wd_mx[c], cols(0, PASS), wd_words[c][:], E4)
@@ -290,13 +290,13 @@ def tile_unifiedautoencodernet_pa_v_kernel(tc, h_enc2, We3, be3, gate_angles, Wd
             vec.tensor_scalar(out=turns_sb[g][:, places], in0=th_sb[g][:, places], scalar1=1.0 / TWO_PI, scalar2=-TILT / TWO_PI,
                               op0=ALU.mult, op1=ALU.add)
 
-        def reduce_angle(g, t, runs=slice(0, 64)):
+        def reduce_angle(g, t, runs=slice(0, 128)):
             if runs.start == 0:
                 reduced_sb[g, t] = sbuf("reduced", [P, NQ], F32, 4)
-            pick = "p j (b t i) -> p t (j b) i"
-            vec.scalar_tensor_tensor(out=reduced_sb[g, t][:].rearrange("p (x i) -> p x i", i=8)[:, runs],
-                                     in0=turns_sb[g][:].rearrange(pick, t=4, i=8)[:, t, runs], scalar=-TWO_PI,
-                                     in1=th_sb[g][:].rearrange(pick, t=4, i=8)[:, t, runs], op0=ALU.mult, op1=ALU.add)
+            pick = "p j (r t i) -> p t (j r) i"
+            vec.scalar_tensor_tensor(out=reduced_sb[g, t][:].rearrange("p (x i) -> p x i", i=4)[:, runs],
+                                     in0=turns_sb[g][:].rearrange(pick, t=4, i=4)[:, t, runs], scalar=-TWO_PI,
+                                     in1=th_sb[g][:].rearrange(pick, t=4, i=4)[:, t, runs], op0=ALU.mult, op1=ALU.add)
 
         def cosine(g, pair):
             folded_sb[g, pair] = sbuf("folded", [P, 2 * PASS], F32)
@@ -360,8 +360,8 @@ def tile_unifiedautoencodernet_pa_v_kernel(tc, h_enc2, We3, be3, gate_angles, Wd
             number, bank = take_bank()
             for x in range(4):
                 pe.transpose(bank[:, cols(x, P)], pairs[:, cols(4 * pair + x, P)], ident[:])
-            dst = token_words[g][:].bitcast(F32).rearrange("p (b t i u) -> p b t i u", t=4, i=8, u=2)
-            act.copy(out=dst[:, :, 2 * pair:2 * pair + 2], in_=bank[:].rearrange("p (t u b i) -> p b t i u", t=2, u=2, i=8))
+            dst = token_words[g][:].bitcast(F32).rearrange("p (r t i u) -> p r t i u", t=4, i=4, u=2)
+            act.copy(out=dst[:, :, 2 * pair:2 * pair + 2], in_=bank[:].rearrange("p (t u r i) -> p r t i u", t=2, u=2, i=4))
             give_bank(number)
 
         def dz1_token_quantize(g):
@@ -415,7 +415,7 @@ def tile_unifiedautoencodernet_pa_v_kernel(tc, h_enc2, We3, be3, gate_angles, Wd
         we_interleave(1)
         for t in range(4):
             for x in range(2):
-                reduce_angle(0, t, cols(x, 32))
+                reduce_angle(0, t, cols(x, 64))
                 issue(WEAVE)
         issue(len(queued))
 

import math
from contextlib import ExitStack

import concourse.mybir as mybir
from concourse.masks import make_identity

B, H2, NQ = 2048, 1024, 512
FLOPS = 3 * 2 * B * H2 * NQ
BYTES = 2 * (2 * B * H2 + 2 * H2 * NQ + 2 * NQ * 3) + 4 * (B * NQ + B * H2) + 4 * (B * H2 + NQ * H2)

F32 = mybir.dt.float32
BF16 = mybir.dt.bfloat16
I32 = mybir.dt.int32
U32 = mybir.dt.uint32
U8 = mybir.dt.uint8
E4 = mybir.dt.float8_e4m3fn_x4
E5 = mybir.dt.float8_e5m2_x4
ALU = mybir.AluOpType
ACT = mybir.ActivationFunctionType

P = 128
PASS = 512
GROUPS = B // PASS
LAST = GROUPS - 1
TWO_PI = 2.0 * math.pi

TILT = 0.6435011087932844
TILT_TAN = 0.75
TILT_COS = 0.8
GUESS_SPAN = 0.999 * math.pi
TINY = 1e-30

LEAD = 9
WEAVE = 2


def tile_unifiedautoencodernet_pa_v_kernel(tc, h_enc2, We3, be3, gate_angles, Wd1, bd1, th, y2, grad_out, out_0, out_1):
    nc = tc.nc
    vec, act, pe = nc.vector, nc.scalar, nc.tensor
    on_vector, on_scalar = vec.tensor_copy, act.copy

    y2_hbm = y2.rearrange("(g p u e) h -> g u p e h", p=P, u=2, e=2)
    grad_hbm = grad_out.rearrange("(g p u e) h -> g u p e h", p=P, u=2, e=2)
    out0_hbm = out_0.rearrange("(g p u e) h -> g u p e h", p=P, u=2, e=2)
    th_hbm = th.rearrange("(g p j) q -> g p j q", p=P, j=4)
    h_hbm = h_enc2.rearrange("(g p j) h -> g p j h", p=P, j=4)
    wd_hbm = Wd1.rearrange("(c p j) q -> c p j q", p=P, j=4)
    we_hbm = We3.rearrange("(r t i) h -> i r t h", t=4, i=4)

    with ExitStack() as ctx:
        sb = ctx.enter_context(tc.tile_pool(name="sb", bufs=1))
        ps = ctx.enter_context(tc.psum_pool(name="ps", bufs=1))
        ctx.enter_context(tc.manual_schedule())

        def sbuf(tag, shape, dtype, bufs=1):
            return sb.tile(shape, dtype, name=tag, tag=tag, bufs=bufs, align_bytes=64)

        def staging(shape, dtype):
            return sbuf("staging", shape, dtype, 5)

        free_banks = list(range(8))

        def take_bank():
            number = free_banks[0]
            free_banks.remove(number)
            return number, ps.tile([P, PASS], F32, name="bank%d" % number, tag="bank%d" % number, bufs=1)

        def give_bank(number):
            free_banks.append(number)

        def cols(n, width):
            return slice(n * width, (n + 1) * width)

        def mx_tiles(tag, width, bufs):
            return sbuf(tag + "_codes", [P, width], U32, bufs), sbuf(tag + "_scales", [P, width], U8, bufs)

        def quantize(dst, window, src, fmt):
            vec.quantize_mx(out=dst[0][:, window].bitcast(fmt), scales=dst[1][:, window], in_=src)

        def mx_pass(bank, lhs, lhs_cols, lhs_fmt, rhs, rhs_cols, rhs_fmt, start, stop):
            pe.matmul_mx(out=bank[:], lhsT=lhs[0][:, lhs_cols].bitcast(lhs_fmt), lhsT_scale=lhs[1][:, lhs_cols],
                         rhs=rhs[0][:, rhs_cols].bitcast(rhs_fmt), rhs_scale=rhs[1][:, rhs_cols], start=start, stop=stop)

        def interleave(copy, dst, src):
            copy(out=dst.rearrange("p (c i t) -> p c t i", i=4, t=4), in_=src.rearrange("p t (c i) -> p c t i", i=4))

        zero_in = sbuf("zero_in", [P, 1], F32)
        vec.memset(zero_in[:], 0.0)
        zero = sbuf("zero", [P, 1], F32)
        act.activation(out=zero[:], in_=zero_in[:], func=ACT.Sin)
        ident = sbuf("ident", [P, P], F32)
        make_identity(nc, ident[:])
        ident_bf = sbuf("ident_bf", [P, P], BF16)
        make_identity(nc, ident_bf[:])

        y2_sb, grad_sb, th_sb, h_sb = {}, {}, {}, {}

        def load_grad(g, u):
            y2_sb[g, u] = sbuf("y2", [P, 2, H2], F32, 3)
            nc.sync.dma_start(out=y2_sb[g, u][:], in_=y2_hbm[g, u])
            grad_sb[g, u] = sbuf("grad", [P, 2, H2], BF16, 4)
            nc.sync.dma_start(out=grad_sb[g, u][:], in_=grad_hbm[g, u])

        def load_th(g):
            th_sb[g] = sbuf("th", [P, 4, NQ], F32, 2)
            nc.sync.dma_start(out=th_sb[g][:], in_=th_hbm[g])

        def load_h(g):
            h_sb[g] = sbuf("h", [P, 4, H2], BF16, 2)
            nc.sync.dma_start(out=h_sb[g][:], in_=h_hbm[g])

        angles_raw = sbuf("angles_raw", [P, 2, 12], BF16)
        nc.sync.dma_start(out=angles_raw[:], in_=gate_angles.rearrange("l (m s) a -> m l (s a)", s=4))
        wd_raw = staging([P, 2, 4, NQ], BF16)
        we_raw = staging([P, 4, H2], BF16)
        nc.sync.dma_start(out=wd_raw[:, 0], in_=wd_hbm[0])
        load_th(0)
        nc.sync.dma_start(out=wd_raw[:, 1], in_=wd_hbm[1])
        for i in range(4):
            nc.sync.dma_start(out=we_raw[i:P:4, :, :], in_=we_hbm[i])
        load_grad(0, 0)
        load_grad(0, 1)
        load_th(1)
        load_grad(1, 0)
        load_h(0)

        small_tags = []

        def small(shape, dtype=F32):
            small_tags.append("small%d" % len(small_tags))
            return sbuf(small_tags[-1], [P] + shape, dtype)

        pick_row = sbuf("pick_row", [P, 4 * P], BF16)
        vec.tensor_copy(out=pick_row[:].rearrange("m (t r i) -> m t r i", t=4, i=4),
                        in_=ident_bf[:].rearrange("m (r t) -> m t r", t=4).unsqueeze(3).to_broadcast([P, 4, 32, 4]))
        pick_qubit = small([4])
        vec.tensor_reduce(out=pick_qubit[:], in_=ident_bf[:].rearrange("p (m s) -> p s m", s=4), axis=mybir.AxisListType.X, op=ALU.add)
        number, bank = take_bank()
        for t in range(4):
            pe.matmul(bank[:, cols(t, 24)], lhsT=pick_row[:, cols(t, P)], rhs=angles_raw[:].rearrange("m l x -> m (l x)"),
                      start=True, stop=True)
        masked = small([8, 4, 3])
        vec.tensor_tensor(out=masked[:], in0=bank[:, 0:96].rearrange("p (x s a) -> p x s a", s=4, a=3),
                          in1=pick_qubit[:].unsqueeze(1).unsqueeze(3).to_broadcast([P, 8, 4, 3]), op=ALU.mult)
        give_bank(number)
        angles_tile = small([8, 3])
        vec.tensor_reduce(out=angles_tile[:], in_=masked[:].rearrange("p x s a -> p x a s"), axis=mybir.AxisListType.X, op=ALU.add)
        angles = angles_tile[:].rearrange("p x a -> p (x a)")

        queued = []

        def tt(a, b, op, shape):
            res = small(shape)[:]
            queued.append(lambda: vec.tensor_tensor(out=res, in0=a, in1=b, op=op))
            return res

        def ts(res, a, s1, s2, op0, op1):
            queued.append(lambda: vec.tensor_scalar(out=res, in0=a, scalar1=s1, scalar2=s2, op0=op0, op1=op1))
            return res

        def stt(res, a, s, b, op0, op1):
            queued.append(lambda: vec.scalar_tensor_tensor(out=res, in0=a, scalar=s, in1=b, op0=op0, op1=op1))
            return res

        def scalar_fn(res, a, func, scale, bias):
            queued.append(lambda: act.activation(out=res, in_=a, func=func, scale=scale, bias=bias))

        def recip(a):
            res = small([4])[:]
            queued.append(lambda: vec.reciprocal(out=res, in_=a))
            return res

        def column():
            return small([4])[:]

        def both(a):
            return a.unsqueeze(1).to_broadcast([P, 2, 4])

        def issue(count):
            for step in queued[:count]:
                step()
                queued.remove(step)

        turns = small([2, 24], I32)
        ts(turns[:, 0, :], angles, 1.0 / TWO_PI, -0.25, ALU.mult, ALU.add)
        ts(turns[:, 1, :], angles, 1.0 / TWO_PI, 0.0, ALU.mult, ALU.add)
        reduced = stt(small([2, 24])[:], turns[:], -TWO_PI, angles.unsqueeze(1).to_broadcast([P, 2, 24]), ALU.mult, ALU.add)
        trig = small([2, 24])
        folded = small([2, 24])
        scalar_fn(folded[:, 0, :], reduced[:, 0, :], ACT.Abs, 1.0, -0.5 * math.pi)
        scalar_fn(folded[:, 1, :], reduced[:, 1, :], ACT.Abs, 1.0, zero[:])
        scalar_fn(trig[:], folded[:], ACT.Sin, -1.0, 0.5 * math.pi)
        trig_steps = len(queued)

        sin_cos = trig[:].rearrange("p w (t l a) -> p l a w t", l=2, a=3)
        rx0, ry0, rz0, rx1, ry1 = sin_cos[:, 0, 0], sin_cos[:, 0, 1], sin_cos[:, 0, 2], sin_cos[:, 1, 0], sin_cos[:, 1, 1]
        yz_rx1 = tt(both(ry1[:, 1]), rx1, ALU.mult, [2, 4])
        x_rz = tt(both(ry1[:, 0]), rz0, ALU.mult, [2, 4])
        y_rz = tt(both(yz_rx1[:, 0]), rz0, ALU.mult, [2, 4])
        z_ry = tt(both(yz_rx1[:, 1]), ry0, ALU.mult, [2, 4])
        x_after_rz = tt(y_rz[:, 0], x_rz[:, 1], ALU.subtract, [4])
        y_after_rz = tt(y_rz[:, 1], x_rz[:, 0], ALU.add, [4])
        x_ry = tt(both(x_after_rz), ry0, ALU.mult, [2, 4])
        y_rx = tt(y_after_rz, rx0[:, 0], ALU.mult, [4])
        z_after_ry = tt(x_ry[:, 0], z_ry[:, 1], ALU.add, [4])
        sa = stt(column(), x_ry[:, 1], TINY, z_ry[:, 0], ALU.add, ALU.subtract)
        z_rx = tt(z_after_ry, rx0[:, 1], ALU.mult, [4])
        ca = tt(z_rx, y_rx, ALU.subtract, [4])

        tilted = small([2, 4])
        tilted_y = stt(tilted[:, 0, :], sa, TILT_TAN, ca, ALU.mult, ALU.add)
        tilted_x = stt(tilted[:, 1, :], ca, -TILT_TAN, sa, ALU.mult, ALU.add)
        magnitude = stt(small([2, 4])[:], tilted[:], -1.0, tilted[:], ALU.mult, ALU.max)
        side = ts(column(), tilted_x, 0.0, GUESS_SPAN, ALU.is_ge, ALU.mult)
        norm = tt(magnitude[:, 0], magnitude[:, 1], ALU.add, [4])
        signed_y = stt(column(), side, -0.5 * GUESS_SPAN, tilted_y, ALU.add, ALU.mult)
        guess = tt(signed_y, recip(norm), ALU.mult, [4])
        guess_trig = small([2, 4])
        scalar_fn(guess_trig[:, 0, :], guess, ACT.Sin, 1.0, 0.0)
        scalar_fn(guess_trig[:, 1, :], guess, ACT.Sin, 1.0, 0.5 * math.pi)
        guess_steps = len(queued) - trig_steps

        y_guess = tt(both(tilted_y), guess_trig[:], ALU.mult, [2, 4])
        x_guess = tt(both(tilted_x), guess_trig[:], ALU.mult, [2, 4])
        along = tt(y_guess[:, 0], x_guess[:, 1], ALU.add, [4])
        across = tt(y_guess[:, 1], x_guess[:, 0], ALU.subtract, [4])
        tangent = tt(across, recip(along), ALU.mult, [4])
        tan_sq = tt(tangent, tangent, ALU.mult, [4])
        atan_1 = ts(column(), tan_sq, -1.0 / 7.0, 1.0 / 5.0, ALU.mult, ALU.add)
        root_1 = ts(column(), tan_sq, TILT_COS / 16.0, -TILT_COS / 8.0, ALU.mult, ALU.add)
        atan_2 = tt(atan_1, tan_sq, ALU.mult, [4])
        root_2 = tt(root_1, tan_sq, ALU.mult, [4])
        atan_3 = stt(column(), atan_2, -1.0 / 3.0, tan_sq, ALU.add, ALU.mult)
        root_3 = stt(column(), root_2, 0.5 * TILT_COS, tan_sq, ALU.add, ALU.mult)
        err = stt(column(), atan_3, 1.0, tangent, ALU.add, ALU.mult)
        phase_amp = small([2, 4])
        amp = stt(phase_amp[:, 1, :], root_3, TILT_COS, along, ALU.add, ALU.mult)
        phase = stt(phase_amp[:, 0, :], guess, -TILT, err, ALU.add, ALU.add)

        wd_mx = [mx_tiles("wd%d" % c, PASS, 1) for c in range(2)]
        we_mx = mx_tiles("we", H2, 1)
        wd_words, we_words = {}, {}

        def wd_interleave(c):
            wd_words[c] = sbuf(("qubit_words", "token_words")[c], [P, 4 * PASS], BF16)
            act.copy(out=wd_words[c][:].rearrange("p (t r i j) -> p t r i j", t=4, i=4, j=4),
                     in_=wd_raw[:, c].rearrange("p j (r t i) -> p t r i j", t=4, i=4))

        def wd_quantize(c):
            quantize(wd_mx[c], cols(0, PASS), wd_words[c][:], E4)

        def we_interleave(n):
            we_words[n] = sbuf("h_words", [P, 4 * PASS], BF16, 2)
            interleave(on_scalar, we_words[n][:], we_raw[:, :, cols(n, PASS)])

        def we_quantize(n):
            quantize(we_mx, cols(n, PASS), we_words[n][:], E4)

        dz2_sb, dz2_words, dz2_mx = {}, {}, {}

        def mask(g, u):
            dz2_sb[g, u] = sbuf("dz2", [P, 2 * H2], BF16, 2)
            vec.scalar_tensor_tensor(out=dz2_sb[g, u][:], in0=y2_sb[g, u][:].rearrange("p e h -> p (e h)"), scalar=0.0,
                                     in1=grad_sb[g, u][:].rearrange("p e h -> p (e h)"), op0=ALU.is_gt, op1=ALU.mult)

        def turn_dz2(g, u):
            pairs = dz2_sb[g, u][:].bitcast(F32)
            for c in range(2):
                if u == 0:
                    dz2_words[g, c] = sbuf("dz2_words", [P, 4 * PASS], BF16, 2)
                number, bank = take_bank()
                for e in range(2):
                    for f in range(2):
                        first = 512 * e + 256 * c
                        pe.transpose(bank[:, cols(2 * e + f, P)], pairs[:, first + f:first + 256:2], ident[:])
                act.copy(out=dz2_words[g, c][:].bitcast(F32)[:, cols(u, PASS)].rearrange("m (p e f) -> m p e f", e=2, f=2),
                         in_=bank[:].rearrange("m (e f p) -> m p e f", e=2, f=2))
                give_bank(number)

        def dz2_quantize(g):
            for c in range(2):
                dz2_mx[g, c] = mx_tiles("dz2", PASS, 2)
                quantize(dz2_mx[g, c], cols(0, PASS), dz2_words[g, c][:], E5)

        turns_sb, reduced_sb, folded_sb, cos_sb, dh_banks, dz1_sb = {}, {}, {}, {}, {}, {}

        def count_turns(g, places=slice(0, 4)):
            if places.start == 0:
                turns_sb[g] = sbuf("turns", [P, 4, NQ], I32)
            vec.tensor_scalar(out=turns_sb[g][:, places], in0=th_sb[g][:, places], scalar1=1.0 / TWO_PI, scalar2=-TILT / TWO_PI,
                              op0=ALU.mult, op1=ALU.add)

        def reduce_angle(g, t, runs=slice(0, 128)):
            if runs.start == 0:
                reduced_sb[g, t] = sbuf("reduced", [P, NQ], F32, 4)
            pick = "p j (r t i) -> p t (j r) i"
            vec.scalar_tensor_tensor(out=reduced_sb[g, t][:].rearrange("p (x i) -> p x i", i=4)[:, runs],
                                     in0=turns_sb[g][:].rearrange(pick, t=4, i=4)[:, t, runs], scalar=-TWO_PI,
                                     in1=th_sb[g][:].rearrange(pick, t=4, i=4)[:, t, runs], op0=ALU.mult, op1=ALU.add)

        def cosine(g, pair):
            folded_sb[g, pair] = sbuf("folded", [P, 2 * PASS], F32)
            for x in range(2):
                t = 2 * pair + x
                number, bank = take_bank()
                for j in range(4):
                    pe.transpose(bank[:, cols(j, P)], reduced_sb[g, t][:, cols(j, P)], ident[:])
                act.activation(out=folded_sb[g, pair][:, cols(x, PASS)].rearrange("q (u p e) -> q u p e", u=2, e=2),
                               in_=bank[:].rearrange("q (u e p) -> q u p e", u=2, e=2), func=ACT.Abs, bias=phase[:, t:t + 1])
                give_bank(number)
            cos_sb[g, pair] = sbuf("cos", [P, 2 * PASS], F32, 2)
            act.activation(out=cos_sb[g, pair][:], in_=folded_sb[g, pair][:], func=ACT.Sin, scale=-1.0, bias=0.5 * math.pi)

        def dh_matmul(g, pair):
            for t in (2 * pair, 2 * pair + 1):
                dh_banks[g, t] = take_bank()
                for c in range(2):
                    mx_pass(dh_banks[g, t][1], wd_mx[c], cols(t, P), E4, dz2_mx[g, c], cols(0, PASS), E5, c == 0, c == 1)

        def make_dz1(g, pair):
            if pair == 0:
                dz1_sb[g] = sbuf("dz1", [P, 4 * PASS], BF16)
            for x in range(2):
                t = 2 * pair + x
                number, bank = dh_banks[g, t]
                vec.scalar_tensor_tensor(out=dz1_sb[g][:, cols(t, PASS)], in0=bank[:], scalar=amp[:, t:t + 1],
                                         in1=cos_sb[g, pair][:, cols(x, PASS)], op0=ALU.mult, op1=ALU.mult)
                give_bank(number)

        h_words, h_mx, qubit_words, token_words, dz1_qubit_mx, dz1_token_mx = {}, {}, {}, {}, {}, {}

        def h_interleave(g, quarter, copy):
            n, x = divmod(quarter, 2)
            if x == 0:
                h_words[g, n] = sbuf("h_words", [P, 4 * PASS], BF16, 2)
            interleave(copy, h_words[g, n][:, cols(x, 1024)], h_sb[g][:, :, cols(quarter, 256)])

        def h_quantize(g):
            h_mx[g] = mx_tiles("h", H2, GROUPS)
            for n in range(2):
                quantize(h_mx[g], cols(n, PASS), h_words[g, n][:], E4)

        def dz1_interleave(g, halves):
            if halves.start == 0:
                qubit_words[g] = sbuf("qubit_words", [P, 4 * PASS], BF16)
            dst = qubit_words[g][:].rearrange("q (u e p t) -> q u e p t", u=2, e=2, t=4)
            src = dz1_sb[g][:].rearrange("q (t u p e) -> q u e p t", t=4, u=2, e=2)
            vec.tensor_copy(out=dst[:, halves], in_=src[:, halves])

        def dz1_qubit_quantize(g, halves):
            if halves.start == 0:
                dz1_qubit_mx[g] = mx_tiles("dz1_qubit", PASS, 1)
            quantize(dz1_qubit_mx[g], slice(256 * halves.start, 256 * halves.stop),
                     qubit_words[g][:, 1024 * halves.start:1024 * halves.stop], E5)

        def turn_dz1(g, pair):
            if pair == 0:
                token_words[g] = sbuf("token_words", [P, 4 * PASS], BF16)
            pairs = dz1_sb[g][:].bitcast(F32)
            number, bank = take_bank()
            for x in range(4):
                pe.transpose(bank[:, cols(x, P)], pairs[:, cols(4 * pair + x, P)], ident[:])
            dst = token_words[g][:].bitcast(F32).rearrange("p (r t i u) -> p r t i u", t=4, i=4, u=2)
            act.copy(out=dst[:, :, 2 * pair:2 * pair + 2], in_=bank[:].rearrange("p (t u r i) -> p r t i u", t=2, u=2, i=4))
            give_bank(number)

        def dz1_token_quantize(g):
            dz1_token_mx[g] = mx_tiles("dz1_token", PASS, GROUPS)
            quantize(dz1_token_mx[g], cols(0, PASS), token_words[g][:], E5)

        out0_sb, out1_banks = {}, {}

        def out0_rows(g, j, copies):
            u, e = divmod(j, 2)
            if e == 0:
                out0_sb[g, u] = staging([P, 2, H2], F32)
            for n in range(2):
                number, bank = take_bank()
                mx_pass(bank, dz1_qubit_mx[g], cols(j, P), E5, we_mx, cols(n, PASS), E4, True, True)
                copies[n](out=out0_sb[g, u][:, e, cols(n, PASS)], in_=bank[:])
                give_bank(number)
            if g == LAST:
                nc.sync.dma_start(out=out0_hbm[g, u][:, e], in_=out0_sb[g, u][:, e])
            elif e == 1:
                nc.sync.dma_start(out=out0_hbm[g, u], in_=out0_sb[g, u][:])

        def out1_open(rows):
            for n in range(2):
                out1_banks[rows, n] = take_bank()
                for g in range(LAST):
                    mx_pass(out1_banks[rows, n][1], dz1_token_mx[g], cols(rows, P), E5, h_mx[g], cols(n, PASS), E4, g == 0, False)

        def out1_close(rows):
            res = staging([P, H2], F32)
            for n in range(2):
                number, bank = out1_banks[rows, n]
                mx_pass(bank, dz1_token_mx[LAST], cols(rows, P), E5, h_mx[LAST], cols(n, PASS), E4, False, True)
                scalar_and_vector[n](out=res[:, cols(n, PASS)], in_=bank[:])
                give_bank(number)
            nc.sync.dma_start(out=out_1[cols(rows, P), :], in_=res[:])

        scalar_only, vector_only, scalar_and_vector = (on_scalar, on_scalar), (on_vector, on_vector), (on_scalar, on_vector)
        both_halves = slice(0, 2)

        issue(trig_steps)
        wd_interleave(0)
        wd_interleave(1)
        issue(LEAD)
        for j in range(4):
            count_turns(0, slice(j, j + 1))
            issue(WEAVE)
        wd_quantize(0)
        issue(guess_steps - LEAD - 4 * WEAVE)
        we_interleave(0)
        we_interleave(1)
        for t in range(4):
            for x in range(2):
                reduce_angle(0, t, cols(x, 64))
                issue(WEAVE)
        issue(len(queued))

        mask(0, 0)
        load_grad(1, 1)
        load_h(1)
        cosine(0, 0)
        turn_dz2(0, 0)
        mask(0, 1)
        load_grad(2, 0)
        cosine(0, 1)
        turn_dz2(0, 1)
        wd_quantize(1)
        we_quantize(0)
        we_quantize(1)
        count_turns(1)
        for t in range(4):
            reduce_angle(1, t)
        dz2_quantize(0)
        dh_matmul(0, 0)
        dh_matmul(0, 1)
        mask(1, 0)
        for quarter in range(4):
            h_interleave(0, quarter, on_scalar)
        load_h(2)
        load_th(2)
        load_grad(2, 1)
        make_dz1(0, 0)
        turn_dz2(1, 0)
        make_dz1(0, 1)
        cosine(1, 0)
        mask(1, 1)
        load_grad(3, 0)
        h_quantize(0)

        for g in range(1, GROUPS):
            if g == 1:
                turn_dz1(0, 0)
                turn_dz1(0, 1)
                turn_dz2(1, 1)
                dz1_interleave(0, both_halves)
                for quarter in range(4):
                    h_interleave(1, quarter, scalar_and_vector[quarter // 2])
                load_h(3)
                load_th(3)
            else:
                for t in range(4):
                    reduce_angle(g, t)
                turn_dz2(g, 1)
                cosine(g, 0)
                dz1_interleave(g - 1, both_halves)
                turn_dz1(g - 1, 0)
                turn_dz1(g - 1, 1)
            cosine(g, 1)
            dz1_qubit_quantize(g - 1, both_halves)
            dz2_quantize(g)
            if g == LAST:
                break
            dh_matmul(g, 0)
            out0_rows(g - 1, 0, scalar_only)
            out0_rows(g - 1, 1, scalar_only)
            mask(g + 1, 0)
            if g + 2 == LAST:
                load_grad(LAST, 1)
            h_quantize(g)
            dz1_token_quantize(g - 1)
            h_interleave(g + 1, 0, on_scalar)
            make_dz1(g, 0)
            turn_dz2(g + 1, 0)
            h_interleave(g + 1, 1, on_scalar)
            dh_matmul(g, 1)
            count_turns(g + 1)
            out0_rows(g - 1, 2, scalar_only)
            out0_rows(g - 1, 3, scalar_only)
            h_interleave(g + 1, 2, on_vector)
            h_interleave(g + 1, 3, on_vector)
            mask(g + 1, 1)
            make_dz1(g, 1)

        out0_rows(LAST - 1, 0, vector_only)
        dh_matmul(LAST, 0)
        h_quantize(LAST)
        dz1_token_quantize(LAST - 1)
        out0_rows(LAST - 1, 1, scalar_only)
        dh_matmul(LAST, 1)
        out0_rows(LAST - 1, 2, scalar_only)
        make_dz1(LAST, 0)
        out0_rows(LAST - 1, 3, scalar_only)
        out1_open(0)
        turn_dz1(LAST, 0)
        make_dz1(LAST, 1)
        turn_dz1(LAST, 1)

        out1_open(1)
        for u in range(2):
            dz1_interleave(LAST, slice(u, u + 1))
        for u in range(2):
            dz1_qubit_quantize(LAST, slice(u, u + 1))
        dz1_token_quantize(LAST)
        out0_rows(LAST, 0, scalar_and_vector)
        out0_rows(LAST, 1, scalar_and_vector)
        out1_close(0)
        out1_close(1)
        out1_open(2)
        out0_rows(LAST, 2, scalar_and_vector)
        out0_rows(LAST, 3, scalar_and_vector)
        out1_close(2)
        out1_open(3)
        out1_close(3)
